import numpy as np
import ml_dtypes


def mxq(x, axis, fmt="e4m3"):
    dtype, down = {"e4m3": (ml_dtypes.float8_e4m3fn, 7), "e5m2": (ml_dtypes.float8_e5m2, 14)}[fmt]
    v = np.moveaxis(np.asarray(x, np.float32).astype(ml_dtypes.bfloat16).astype(np.float64), axis, -1)
    blocks = v.reshape(v.shape[:-1] + (-1, 32))
    amax = np.abs(blocks).max(-1, keepdims=True)
    byte = np.maximum(np.where(amax > 0, np.frexp(amax)[1] - 1 + 127, 0) - down, 1)
    scale = np.exp2(byte - 127.0)
    codes = (blocks / scale).astype(np.float32).astype(dtype).astype(np.float64)
    return np.moveaxis((codes * scale).reshape(v.shape), -1, axis)


WIDE = False


def mx_kscale(k):
    if not WIDE:
        return np.ones(k)
    levels = np.array([10, -10, 5, -5, 0])
    if k % 512:
        return np.exp2(np.random.permutation(np.resize(levels, k // 32))).repeat(32)
    a = np.empty((k // 512, 16))
    for p in range(k // 512):
        a[p, :8] = np.random.permutation(np.resize(levels, 8))
        for g in range(8):
            far = levels[np.abs(levels - a[p, g]) >= 10]
            a[p, g + 8] = far[np.random.randint(len(far))]
    return np.exp2(a.ravel()).repeat(32)


BF16 = ml_dtypes.bfloat16


def bf(x):
    return np.asarray(x, np.float32).astype(BF16)


def f64(x):
    return np.asarray(x).astype(np.float64)


B, T, E, C, H, XB = 1, 512, 2048, 2048, 16, 512
SCALE_BASE = float(XB)


def rotate_every_two(z):
    z1 = z[..., ::2]
    z2 = z[..., 1::2]
    return np.stack([-z2, z1], axis=-1).reshape(z.shape)


def xpos(z):
    dim_scale = (f64(np.arange(0, C, 2)) + 0.4 * C) / (1.4 * C)
    pos = f64(np.arange(T))
    scale = dim_scale[None, :] ** (pos[:, None] / SCALE_BASE)
    inv_freq = 1.0 / (10000.0 ** (f64(np.arange(0, C, 2)) / C))
    sinusoid = pos[:, None] * inv_freq[None, :]
    sin = np.repeat(np.sin(sinusoid) * scale, 2, axis=-1)
    cos = np.repeat(np.cos(sinusoid) * scale, 2, axis=-1)
    return z * cos[None] + rotate_every_two(z) * sin[None]


def draw0():
    s = mx_kscale(E)
    return {"x": bf(np.random.standard_normal((B, T, E)) * s),
            "w_q": bf(np.random.standard_normal((E, C)) * 0.5 / np.sqrt(E) / s[:, None]),
            "w_k": bf(np.random.standard_normal((E, C)) * 0.5 / np.sqrt(E) / s[:, None])}


def core(x, w_q, w_k):
    xq = mxq(f64(x), 2, "e4m3")
    q = xq @ mxq(f64(w_q), 0, "e4m3")
    k = xq @ mxq(f64(w_k), 0, "e4m3")
    return xpos(q), xpos(k)


def e4m3fn_bytes(y):
    return np.clip(np.asarray(y, np.float64), -448.0, 448.0).astype(np.float32).astype(ml_dtypes.float8_e4m3fn).view(np.uint8)


def e4m3fn_values(b):
    return np.asarray(b, np.uint8).view(ml_dtypes.float8_e4m3fn).astype(np.float64)


def setup_inputs():
    d = draw0()
    x0 = np.asarray(d['w_q']).astype(np.float64)
    s = (np.max(np.abs(x0), axis=(1,), keepdims=True) / 448.0).astype(np.float32)
    out = {}
    for k, v in d.items():
        if k == 'w_q':
            out['w_q_bytes'] = e4m3fn_bytes(x0 / s.astype(np.float64))
            out['w_q_scale'] = s
        else:
            out[k] = v
    return out


def reference(x, w_q_bytes, w_q_scale, w_k):
    return core(x, e4m3fn_values(w_q_bytes) * w_q_scale.astype(np.float64), w_k)

@@ -1,0 +1,210 @@
+from contextlib import ExitStack
+import math
+
+import concourse.mybir as mybir
+from concourse.masks import make_identity
+
+T, E, C = 512, 2048, 2048
+FLOPS = 2 * 2 * T * E * C
+
+F32 = mybir.dt.float32
+BF16 = mybir.dt.bfloat16
+U32 = mybir.dt.uint32
+I32 = mybir.dt.int32
+U8 = mybir.dt.uint8
+FP8 = mybir.dt.float8_e4m3fn
+FP8X4 = mybir.dt.float8_e4m3fn_x4
+ACT = mybir.ActivationFunctionType
+ALU = mybir.AluOpType
+
+P = 128
+PACK = 4
+K_PASS = P * PACK
+PASSES = E // K_PASS
+MT = T // P
+NCH = 512
+CHUNKS = C // NCH
+PAIRS = C // 2
+JCH = NCH // 2
+
+ORDER = ["k0","q0","k1","q1","k2","q2","k3","q3"]
+HOW = ["TTTA","AAAA","TTTA","AAAA","TTTA","AAAA","TTTA","AAAA"]
+ADD = ["GGGV","GGGV","GGGV","GGGV","GGGV","GGGV","GGGV","GGGV"]
+XCOPY = "VVVVVVVV"
+FAST = False
+
+
+def tile_multiscaleretention_pa_kernel(tc, x, w_q_bytes, w_q_scale, w_k, out_0, out_1):
+    nc = tc.nc
+    with ExitStack() as ctx:
+        const = ctx.enter_context(tc.tile_pool(name="const", bufs=1))
+        tmp = ctx.enter_context(tc.tile_pool(name="tmp", bufs=2))
+        xgp = ctx.enter_context(tc.tile_pool(name="xgp", bufs=2))
+        wkp = ctx.enter_context(tc.tile_pool(name="wkp", bufs=6))
+        wqp = ctx.enter_context(tc.tile_pool(name="wqp", bufs=6))
+        widep = ctx.enter_context(tc.tile_pool(name="widep", bufs=3))
+        grp = ctx.enter_context(tc.tile_pool(name="grp", bufs=4))
+        cdp = ctx.enter_context(tc.tile_pool(name="cdp", bufs=8))
+        epp = ctx.enter_context(tc.tile_pool(name="epp", bufs=3))
+        psum = ctx.enter_context(tc.psum_pool(name="psum", bufs=6))
+
+        xraw = []
+        for m in range(MT):
+            xr = const.tile([P, E], BF16, name="xraw%d" % m)
+            nc.sync.dma_start(out=xr[:], in_=x[0, m * P:(m + 1) * P, :])
+            xraw.append(xr)
+        wqs = const.tile([P, PASSES, PACK], F32, name="wqs")
+        nc.sync.dma_start(out=wqs[:], in_=w_q_scale.rearrange("(g p t) o -> p g (t o)", p=P, t=PACK))
+
+        jidx = const.tile([P, PAIRS], F32, name="jidx")
+        nc.gpsimd.iota(jidx[:], pattern=[[1, PAIRS]], base=0, channel_multiplier=0,
+                       allow_small_or_imprecise_dtypes=True)
+        tpos = const.tile([P, MT], F32, name="tpos")
+        nc.gpsimd.iota(tpos[:], pattern=[[P, MT]], base=0, channel_multiplier=1,
+                       allow_small_or_imprecise_dtypes=True)
+        ident = const.tile([P, P], F32, name="ident")
+        make_identity(nc, ident[:])
+        identb = const.tile([P, P], BF16, name="identb")
+        make_identity(nc, identb[:])
+
+        lnd = const.tile([P, PAIRS], F32, name="lnd")
+        nc.scalar.activation(out=lnd[:], in_=jidx[:], func=ACT.Ln, scale=2.0 / (1.4 * C), bias=0.4 * C / (1.4 * C))
+
+        tturn = const.tile([P, MT], F32, name="tturn")
+        nc.vector.tensor_scalar(out=tturn[:], in0=tpos[:], scalar1=1.0 / (2.0 * math.pi), scalar2=None, op0=ALU.mult)
+        t512 = const.tile([P, MT], F32, name="t512")
+        nc.vector.tensor_scalar(out=t512[:], in0=tpos[:], scalar1=1.0 / 512.0, scalar2=None, op0=ALU.mult)
+        tneg = const.tile([P, MT], F32, name="tneg")
+        nc.vector.tensor_scalar(out=tneg[:], in0=tpos[:], scalar1=-1.0, scalar2=None, op0=ALU.mult)
+
+        freq = const.tile([P, PAIRS], F32, name="freq")
+        nc.vector.memset(freq[:, 0:1], 1.0)
+        for lv in range(10):
+            w = 1 << lv
+            nc.vector.tensor_scalar(out=freq[:, w:2 * w], in0=freq[:, 0:w],
+                                    scalar1=pow(10000.0, -w / float(PAIRS)), scalar2=None, op0=ALU.mult)
+
+        ctab = []
+        stab = []
+        for m in range(MT):
+            ct = const.tile([P, PAIRS], F32, name="ctab%d" % m)
+            st = const.tile([P, 2, PAIRS], F32, name="stab%d" % m)
+            ctab.append(ct)
+            stab.append(st)
+            nc.scalar.activation(out=ct[:], in_=lnd[:], func=ACT.Exp, scale=t512[:, m:m + 1])
+
+        for m in range(MT):
+            ct, st = ctab[m], stab[m]
+            tmax = m * P + P - 1
+            j0 = int(math.ceil(PAIRS * math.log(tmax / 3.14) / math.log(10000.0) / 32.0)) * 32
+            nturn = tmp.tile([P, PAIRS], I32, tag="nturn")
+            nc.vector.tensor_scalar(out=nturn[:, 0:j0], in0=freq[:, 0:j0], scalar1=tturn[:, m:m + 1], scalar2=None,
+                                    op0=ALU.mult)
+            frac = tmp.tile([P, PAIRS], F32, tag="frac")
+            nc.vector.scalar_tensor_tensor(out=frac[:, 0:j0], in0=freq[:, 0:j0], scalar=tturn[:, m:m + 1],
+                                           in1=nturn[:, 0:j0], op0=ALU.mult, op1=ALU.subtract)
+            cosv = tmp.tile([P, PAIRS], F32, tag="cosv")
+            nc.scalar.activation(out=st[:, 0, j0:], in_=freq[:, j0:], func=ACT.Sin, scale=tpos[:, m:m + 1])
+            nc.scalar.activation(out=cosv[:, j0:], in_=freq[:, j0:], func=ACT.Sin, scale=tneg[:, m:m + 1],
+                                 bias=0.5 * math.pi)
+            nc.scalar.activation(out=st[:, 0, 0:j0], in_=frac[:, 0:j0], func=ACT.Sin, scale=2.0 * math.pi)
+            afr = tmp.tile([P, PAIRS], F32, tag="afr")
+            nc.scalar.activation(out=afr[:, 0:j0], in_=frac[:, 0:j0], func=ACT.Abs)
+            nc.scalar.activation(out=cosv[:, 0:j0], in_=afr[:, 0:j0], func=ACT.Sin, scale=-2.0 * math.pi,
+                                 bias=0.5 * math.pi)
+            nc.vector.tensor_tensor(out=st[:, 0, :], in0=st[:, 0, :], in1=ct[:], op=ALU.mult)
+            nc.vector.tensor_scalar(out=st[:, 1, :], in0=st[:, 0, :], scalar1=-1.0, scalar2=None, op0=ALU.mult)
+            nc.vector.tensor_tensor(out=ct[:], in0=cosv[:], in1=ct[:], op=ALU.mult)
+
+        xcodes = []
+        xscl = []
+        for m in range(MT):
+            words = xraw[m][:].bitcast(F32)
+            xg = xgp.tile([P, PASSES * P * PACK], BF16, tag="xg", align_bytes=64)
+            xgw = xg[:].bitcast(F32).rearrange("p (g r u) -> p g r u", g=PASSES, r=P, u=2)
+            for h in range(2):
+                xt = psum.tile([P, 2, 2, P], F32, tag="acc")
+                for gg in range(2):
+                    g = 2 * h + gg
+                    for u in range(2):
+                        nc.tensor.transpose(xt[:, gg, u, :], words[:, 256 * g + u:256 * (g + 1):2], ident[:])
+                if XCOPY[2 * m + h] == "S":
+                    nc.scalar.copy(out=xgw[:, 2 * h:2 * h + 2], in_=xt[:].rearrange("p g u r -> p g r u"))
+                else:
+                    nc.vector.tensor_copy(out=xgw[:, 2 * h:2 * h + 2], in_=xt[:].rearrange("p g u r -> p g r u"))
+            xc = const.tile([P, PASSES * P], U32, name="xc%d" % m, align_bytes=64)
+            xs = const.tile([P, PASSES * P], U8, name="xs%d" % m, align_bytes=64)
+            nc.vector.quantize_mx(out=xc[:].bitcast(FP8X4), scales=xs[:], in_=xg[:])
+            xcodes.append(xc)
+            xscl.append(xs)
+
+        for pos in range(len(ORDER)):
+            kind = ORDER[pos][0]
+            c = int(ORDER[pos][1])
+            cols = slice(c * NCH, (c + 1) * NCH)
+            js = slice(c * JCH, (c + 1) * JCH)
+            dst = out_0 if kind == "q" else out_1
+            wc = []
+            for g in range(PASSES):
+                rows = slice(g * K_PASS, (g + 1) * K_PASS)
+                if kind == "k":
+                    src = wkp.tile([P, PACK, NCH], BF16, tag="wk")
+                    nc.sync.dma_start(out=src[:], in_=w_k[rows, cols].rearrange("(p t) n -> p t n", t=PACK))
+                else:
+                    byt = wqp.tile([P, PACK, NCH], U8, tag="wqb")
+                    nc.sync.dma_start(out=byt[:], in_=w_q_bytes[rows, cols].rearrange("(p t) n -> p t n", t=PACK))
+                    src = widep.tile([P, PACK, NCH], BF16, tag="wide")
+                    for t in range(PACK):
+                        nc.scalar.activation(out=src[:, t, :], in_=byt[:, t, :].bitcast(FP8), func=ACT.Copy,
+                                             scale=wqs[:, g, t:t + 1])
+                grouped = grp.tile([P, NCH, PACK], BF16, tag="grouped", align_bytes=64)
+                how = HOW[pos][g]
+                if FAST:
+                    gdst = grouped[:].rearrange("p (c i) t -> p c t i", i=4)
+                    gsrc = src[:].rearrange("p t (c i) -> p c t i", i=4)
+                else:
+                    gdst = grouped[:]
+                    gsrc = src[:].rearrange("p t c -> p c t")
+                if how == "S":
+                    nc.scalar.copy(out=gdst, in_=gsrc)
+                elif how == "V":
+                    nc.vector.tensor_copy(out=gdst, in_=gsrc)
+                elif how == "A":
+                    nc.any.tensor_copy(out=gdst, in_=gsrc)
+                else:
+                    gflat = grouped[:].rearrange("p c t -> p (c t)")
+                    for hb in range(2):
+                        pt = psum.tile([P, 1024], BF16, tag="pt", bufs=2)
+                        for q4 in range(2):
+                            c0 = hb * 256 + q4 * 128
+                            nc.tensor.matmul(out=pt[:, q4 * 512:(q4 + 1) * 512], lhsT=identb[:],
+                                             rhs=src[:, :, c0:c0 + 128].rearrange("p t c -> p c t"),
+                                             start=True, stop=True)
+                        nc.scalar.copy(out=gflat[:, hb * 1024:(hb + 1) * 1024], in_=pt[:])
+                codes = cdp.tile([P, NCH], U32, tag="codes", align_bytes=64)
+                scl = cdp.tile([P, NCH], U8, tag="scl", align_bytes=64)
+                nc.vector.quantize_mx(out=codes[:].bitcast(FP8X4), scales=scl[:],
+                                      in_=grouped[:].rearrange("p c t -> p (c t)"))
+                wc.append((codes, scl))
+
+            for m in range(MT):
+                acc = psum.tile([P, NCH], F32, tag="acc")
+                for g in range(PASSES):
+                    codes, scl = wc[g]
+                    nc.tensor.matmul_mx(out=acc[:],
+                                        lhsT=xcodes[m][:, g * P:(g + 1) * P].bitcast(FP8X4),
+                                        lhsT_scale=xscl[m][:, g * P:(g + 1) * P],
+                                        rhs=codes[:].bitcast(FP8X4), rhs_scale=scl[:],
+                                        start=(g == 0), stop=(g == PASSES - 1))
+                z = acc[:].rearrange("p (j e) -> p e j", e=2)
+                t1 = epp.tile([P, 2, JCH], F32, tag="t1")
+                nc.vector.tensor_tensor(out=t1[:], in0=z, in1=ctab[m][:, js].unsqueeze(1).to_broadcast([P, 2, JCH]),
+                                        op=ALU.mult)
+                t2 = epp.tile([P, 2, JCH], F32, tag="t2")
+                nc.vector.tensor_tensor(out=t2[:], in0=z, in1=stab[m][:, :, js], op=ALU.mult)
+                o = epp.tile([P, NCH], F32, tag="o")
+                adder = nc.gpsimd if ADD[pos][m] == "G" else nc.vector
+                adder.tensor_tensor(out=o[:].rearrange("p (j e) -> p j e", e=2),
+                                    in0=t1[:].rearrange("p e j -> p j e"),
+                                    in1=t2[:, ::-1, :].rearrange("p e j -> p j e"), op=ALU.add)
+                nc.sync.dma_start(out=dst[0, m * P:(m + 1) * P, cols], in_=o[:])

@@ -16,6 +16,7 @@ FP8 = mybir.dt.float8_e4m3fn
 FP8X4 = mybir.dt.float8_e4m3fn_x4
 ACT = mybir.ActivationFunctionType
 ALU = mybir.AluOpType
+ENG = mybir.EngineType
 
 P = 128
 PACK = 4
@@ -23,188 +24,333 @@ K_PASS = P * PACK
 PASSES = E // K_PASS
 MT = T // P
 NCH = 512
-CHUNKS = C // NCH
 PAIRS = C // 2
 JCH = NCH // 2
+JRED = 576
 
 ORDER = ["k0","q0","k1","q1","k2","q2","k3","q3"]
-HOW = ["TTTA","AAAA","TTTA","AAAA","TTTA","AAAA","TTTA","AAAA"]
-ADD = ["GGGV","GGGV","GGGV","GGGV","GGGV","GGGV","GGGV","GGGV"]
-XCOPY = "VVVVVVVV"
-FAST = False
+HOW = ["VVVV","PPVV","PPVS","PVSS","PPVS","PVSS","PPSS","PSSS"]
+ADD = ["GGGG","GGGG","GGGG","GGGG","GGGG","GGGG","GGGG","GGGV"]
+XCOPY = "SSSSSSSS"
+TM_AT = [[9,9],[9,9],[9,9],[9,9]]
+NPOS = len(ORDER)
 
 
 def tile_multiscaleretention_pa_kernel(tc, x, w_q_bytes, w_q_scale, w_k, out_0, out_1):
     nc = tc.nc
     with ExitStack() as ctx:
+        ctx.enter_context(tc.manual_schedule(engines={ENG.DVE, ENG.Pool, ENG.Activation, ENG.PE}))
         const = ctx.enter_context(tc.tile_pool(name="const", bufs=1))
-        tmp = ctx.enter_context(tc.tile_pool(name="tmp", bufs=2))
-        xgp = ctx.enter_context(tc.tile_pool(name="xgp", bufs=2))
         wkp = ctx.enter_context(tc.tile_pool(name="wkp", bufs=6))
         wqp = ctx.enter_context(tc.tile_pool(name="wqp", bufs=6))
-        widep = ctx.enter_context(tc.tile_pool(name="widep", bufs=3))
-        grp = ctx.enter_context(tc.tile_pool(name="grp", bufs=4))
+        widep = ctx.enter_context(tc.tile_pool(name="widep", bufs=4))
+        grp = ctx.enter_context(tc.tile_pool(name="grp", bufs=6))
         cdp = ctx.enter_context(tc.tile_pool(name="cdp", bufs=8))
-        epp = ctx.enter_context(tc.tile_pool(name="epp", bufs=3))
-        psum = ctx.enter_context(tc.psum_pool(name="psum", bufs=6))
+        psum = ctx.enter_context(tc.psum_pool(name="psum", bufs=4))
+        late = {}
 
-        xraw = []
-        for m in range(MT):
-            xr = const.tile([P, E], BF16, name="xraw%d" % m)
-            nc.sync.dma_start(out=xr[:], in_=x[0, m * P:(m + 1) * P, :])
-            xraw.append(xr)
-        wqs = const.tile([P, PASSES, PACK], F32, name="wqs")
-        nc.sync.dma_start(out=wqs[:], in_=w_q_scale.rearrange("(g p t) o -> p g (t o)", p=P, t=PACK))
+        raw = {}
+        wide = {}
+        grouped = {}
+        ptiles = {}
+        wcodes = {}
+        accs = {}
+        prods = {}
 
-        jidx = const.tile([P, PAIRS], F32, name="jidx")
-        nc.gpsimd.iota(jidx[:], pattern=[[1, PAIRS]], base=0, channel_multiplier=0,
-                       allow_small_or_imprecise_dtypes=True)
-        tpos = const.tile([P, MT], F32, name="tpos")
-        nc.gpsimd.iota(tpos[:], pattern=[[P, MT]], base=0, channel_multiplier=1,
-                       allow_small_or_imprecise_dtypes=True)
-        ident = const.tile([P, P], F32, name="ident")
-        make_identity(nc, ident[:])
-        identb = const.tile([P, P], BF16, name="identb")
-        make_identity(nc, identb[:])
+        def kind(pos):
+            return ORDER[pos][0]
 
-        lnd = const.tile([P, PAIRS], F32, name="lnd")
-        nc.scalar.activation(out=lnd[:], in_=jidx[:], func=ACT.Ln, scale=2.0 / (1.4 * C), bias=0.4 * C / (1.4 * C))
-
-        tturn = const.tile([P, MT], F32, name="tturn")
-        nc.vector.tensor_scalar(out=tturn[:], in0=tpos[:], scalar1=1.0 / (2.0 * math.pi), scalar2=None, op0=ALU.mult)
-        t512 = const.tile([P, MT], F32, name="t512")
-        nc.vector.tensor_scalar(out=t512[:], in0=tpos[:], scalar1=1.0 / 512.0, scalar2=None, op0=ALU.mult)
-        tneg = const.tile([P, MT], F32, name="tneg")
-        nc.vector.tensor_scalar(out=tneg[:], in0=tpos[:], scalar1=-1.0, scalar2=None, op0=ALU.mult)
-
-        freq = const.tile([P, PAIRS], F32, name="freq")
-        nc.vector.memset(freq[:, 0:1], 1.0)
-        for lv in range(10):
-            w = 1 << lv
-            nc.vector.tensor_scalar(out=freq[:, w:2 * w], in0=freq[:, 0:w],
-                                    scalar1=pow(10000.0, -w / float(PAIRS)), scalar2=None, op0=ALU.mult)
-
-        ctab = []
-        stab = []
-        for m in range(MT):
-            ct = const.tile([P, PAIRS], F32, name="ctab%d" % m)
-            st = const.tile([P, 2, PAIRS], F32, name="stab%d" % m)
-            ctab.append(ct)
-            stab.append(st)
-            nc.scalar.activation(out=ct[:], in_=lnd[:], func=ACT.Exp, scale=t512[:, m:m + 1])
-
-        for m in range(MT):
-            ct, st = ctab[m], stab[m]
-            tmax = m * P + P - 1
-            j0 = int(math.ceil(PAIRS * math.log(tmax / 3.14) / math.log(10000.0) / 32.0)) * 32
-            nturn = tmp.tile([P, PAIRS], I32, tag="nturn")
-            nc.vector.tensor_scalar(out=nturn[:, 0:j0], in0=freq[:, 0:j0], scalar1=tturn[:, m:m + 1], scalar2=None,
-                                    op0=ALU.mult)
-            frac = tmp.tile([P, PAIRS], F32, tag="frac")
-            nc.vector.scalar_tensor_tensor(out=frac[:, 0:j0], in0=freq[:, 0:j0], scalar=tturn[:, m:m + 1],
-                                           in1=nturn[:, 0:j0], op0=ALU.mult, op1=ALU.subtract)
-            cosv = tmp.tile([P, PAIRS], F32, tag="cosv")
-            nc.scalar.activation(out=st[:, 0, j0:], in_=freq[:, j0:], func=ACT.Sin, scale=tpos[:, m:m + 1])
-            nc.scalar.activation(out=cosv[:, j0:], in_=freq[:, j0:], func=ACT.Sin, scale=tneg[:, m:m + 1],
-                                 bias=0.5 * math.pi)
-            nc.scalar.activation(out=st[:, 0, 0:j0], in_=frac[:, 0:j0], func=ACT.Sin, scale=2.0 * math.pi)
-            afr = tmp.tile([P, PAIRS], F32, tag="afr")
-            nc.scalar.activation(out=afr[:, 0:j0], in_=frac[:, 0:j0], func=ACT.Abs)
-            nc.scalar.activation(out=cosv[:, 0:j0], in_=afr[:, 0:j0], func=ACT.Sin, scale=-2.0 * math.pi,
-                                 bias=0.5 * math.pi)
-            nc.vector.tensor_tensor(out=st[:, 0, :], in0=st[:, 0, :], in1=ct[:], op=ALU.mult)
-            nc.vector.tensor_scalar(out=st[:, 1, :], in0=st[:, 0, :], scalar1=-1.0, scalar2=None, op0=ALU.mult)
-            nc.vector.tensor_tensor(out=ct[:], in0=cosv[:], in1=ct[:], op=ALU.mult)
-
-        xcodes = []
-        xscl = []
-        for m in range(MT):
-            words = xraw[m][:].bitcast(F32)
-            xg = xgp.tile([P, PASSES * P * PACK], BF16, tag="xg", align_bytes=64)
-            xgw = xg[:].bitcast(F32).rearrange("p (g r u) -> p g r u", g=PASSES, r=P, u=2)
-            for h in range(2):
-                xt = psum.tile([P, 2, 2, P], F32, tag="acc")
-                for gg in range(2):
-                    g = 2 * h + gg
-                    for u in range(2):
-                        nc.tensor.transpose(xt[:, gg, u, :], words[:, 256 * g + u:256 * (g + 1):2], ident[:])
-                if XCOPY[2 * m + h] == "S":
-                    nc.scalar.copy(out=xgw[:, 2 * h:2 * h + 2], in_=xt[:].rearrange("p g u r -> p g r u"))
-                else:
-                    nc.vector.tensor_copy(out=xgw[:, 2 * h:2 * h + 2], in_=xt[:].rearrange("p g u r -> p g r u"))
-            xc = const.tile([P, PASSES * P], U32, name="xc%d" % m, align_bytes=64)
-            xs = const.tile([P, PASSES * P], U8, name="xs%d" % m, align_bytes=64)
-            nc.vector.quantize_mx(out=xc[:].bitcast(FP8X4), scales=xs[:], in_=xg[:])
-            xcodes.append(xc)
-            xscl.append(xs)
-
-        for pos in range(len(ORDER)):
-            kind = ORDER[pos][0]
+        def cols(pos):
             c = int(ORDER[pos][1])
-            cols = slice(c * NCH, (c + 1) * NCH)
-            js = slice(c * JCH, (c + 1) * JCH)
-            dst = out_0 if kind == "q" else out_1
-            wc = []
+            return slice(c * NCH, (c + 1) * NCH)
+
+        def load(pos, g):
+            rows = slice(g * K_PASS, (g + 1) * K_PASS)
+            if kind(pos) == "k":
+                t = wkp.tile([P, PACK, NCH], BF16, tag="wk")
+                nc.sync.dma_start(out=t[:], in_=w_k[rows, cols(pos)].rearrange("(p t) n -> p t n", t=PACK))
+                wide[(pos, g)] = t
+            else:
+                t = wqp.tile([P, PACK, NCH], U8, tag="wqb")
+                nc.sync.dma_start(out=t[:], in_=w_q_bytes[rows, cols(pos)].rearrange("(p t) n -> p t n", t=PACK))
+                raw[(pos, g)] = t
+
+        def widen(pos, g):
+            if kind(pos) == "q":
+                t = widep.tile([P, PACK, NCH], BF16, tag="wide")
+                for j in range(PACK):
+                    nc.scalar.activation(out=t[:, j, :], in_=raw[(pos, g)][:, j, :].bitcast(FP8), func=ACT.Copy,
+                                         scale=wqs[:, g, j:j + 1])
+                wide[(pos, g)] = t
+
+        def new_grouped(pos, g, eng):
+            if eng == "S":
+                t = grp.tile([P, NCH, PACK], BF16, tag="gs", align_bytes=64)
+            else:
+                t = grp.tile([P, NCH, PACK], BF16, tag="gv", align_bytes=64, bufs=3)
+            grouped[(pos, g)] = t
+            return t
+
+        def inter(pos, g, eng):
+            t = new_grouped(pos, g, eng)
+            if eng == "S":
+                nc.scalar.copy(out=t[:], in_=wide[(pos, g)][:].rearrange("p t c -> p c t"))
+            else:
+                nc.vector.tensor_copy(out=t[:], in_=wide[(pos, g)][:].rearrange("p t c -> p c t"))
+
+        def pt_mm(pos, g):
+            for hb in range(2):
+                pt = psum.tile([P, 1024], BF16, tag="pt", bufs=4)
+                for q4 in range(2):
+                    c0 = hb * 256 + q4 * 128
+                    nc.tensor.matmul(out=pt[:, q4 * 512:(q4 + 1) * 512], lhsT=identb[:],
+                                     rhs=wide[(pos, g)][:, :, c0:c0 + 128].rearrange("p t c -> p c t"),
+                                     start=True, stop=True)
+                ptiles[(pos, g, hb)] = pt
+
+        def pt_evac(pos, g, eng):
+            t = new_grouped(pos, g, eng)
+            flat = t[:].rearrange("p c t -> p (c t)")
+            for hb in range(2):
+                if eng == "S":
+                    nc.scalar.copy(out=flat[:, hb * 1024:(hb + 1) * 1024], in_=ptiles[(pos, g, hb)][:])
+                else:
+                    nc.vector.tensor_copy(out=flat[:, hb * 1024:(hb + 1) * 1024], in_=ptiles[(pos, g, hb)][:])
+
+        def quant(pos, g):
+            codes = cdp.tile([P, NCH], U32, tag="codes", align_bytes=64)
+            scl = cdp.tile([P, NCH], U8, tag="scl", align_bytes=64)
+            nc.vector.quantize_mx(out=codes[:].bitcast(FP8X4), scales=scl[:],
+                                  in_=grouped[(pos, g)][:].rearrange("p c t -> p (c t)"))
+            wcodes[(pos, g)] = (codes, scl)
+
+        def mm(pos, m):
+            acc = psum.tile([P, NCH], F32, tag="acc")
             for g in range(PASSES):
-                rows = slice(g * K_PASS, (g + 1) * K_PASS)
-                if kind == "k":
-                    src = wkp.tile([P, PACK, NCH], BF16, tag="wk")
-                    nc.sync.dma_start(out=src[:], in_=w_k[rows, cols].rearrange("(p t) n -> p t n", t=PACK))
+                codes, scl = wcodes[(pos, g)]
+                nc.tensor.matmul_mx(out=acc[:],
+                                    lhsT=xcodes[m][:, g * P:(g + 1) * P].bitcast(FP8X4),
+                                    lhsT_scale=xscl[m][:, g * P:(g + 1) * P],
+                                    rhs=codes[:].bitcast(FP8X4), rhs_scale=scl[:],
+                                    start=(g == 0), stop=(g == PASSES - 1))
+            accs[(pos, m)] = acc
+
+        def ep12(pos, m):
+            epp = late["epp"]
+            c = int(ORDER[pos][1])
+            js = slice(c * JCH, (c + 1) * JCH)
+            z = accs[(pos, m)][:].rearrange("p (j e) -> p e j", e=2)
+            t1 = epp.tile([P, 2, JCH], F32, tag="t1")
+            nc.vector.tensor_tensor(out=t1[:], in0=z, in1=ctab[m][:, js].unsqueeze(1).to_broadcast([P, 2, JCH]),
+                                    op=ALU.mult)
+            t2 = epp.tile([P, 2, JCH], F32, tag="t2")
+            nc.vector.tensor_tensor(out=t2[:], in0=z, in1=stab[m][:, :, js], op=ALU.mult)
+            prods[(pos, m)] = (t1, t2)
+
+        def ep3(pos, m):
+            epp = late["epp"]
+            t1, t2 = prods[(pos, m)]
+            dst = out_0 if kind(pos) == "q" else out_1
+            o = epp.tile([P, NCH], F32, tag="o")
+            adder = nc.gpsimd if ADD[pos][m] == "G" else nc.vector
+            adder.tensor_tensor(out=o[:].rearrange("p (j e) -> p j e", e=2),
+                                in0=t1[:].rearrange("p e j -> p j e"),
+                                in1=t2[:, ::-1, :].rearrange("p e j -> p j e"), op=ALU.add)
+            nc.sync.dma_start(out=dst[0, m * P:(m + 1) * P, cols(pos)], in_=o[:])
+
+        def s_tasks(pos):
+            for g in range(PASSES):
+                widen(pos, g)
+                if HOW[pos][g] in "PT":
+                    pt_mm(pos, g)
+            for g in range(PASSES):
+                if HOW[pos][g] == "T":
+                    pt_evac(pos, g, "S")
+                elif HOW[pos][g] == "S":
+                    inter(pos, g, "S")
+
+        def part_a(s):
+            if s < NPOS:
+                for g in range(PASSES):
+                    if HOW[s][g] == "P":
+                        pt_evac(s, g, "V")
+            if s + 2 < NPOS:
+                load(s + 2, 0)
+                load(s + 2, 1)
+            if 1 <= s and s + 1 < NPOS:
+                s_tasks(s + 1)
+            if s < NPOS:
+                ready = [g for g in range(PASSES) if HOW[s][g] in "ST"] + [g for g in range(PASSES) if HOW[s][g] == "P"]
+                for g in range(PASSES):
+                    if HOW[s][g] == "V":
+                        inter(s, g, "V")
+                        if ready:
+                            quant(s, ready.pop(0))
+                        ready.append(g)
+                if s + 2 < NPOS:
+                    load(s + 2, 2)
+                    load(s + 2, 3)
+                if s == 0:
+                    for m in range(MT):
+                        x_quant(m)
+                for g in ready:
+                    quant(s, g)
+
+        def part_b(s):
+            for m in range(MT):
+                if s >= 1:
+                    ep12(s - 1, m)
+                    if m >= 1:
+                        ep3(s - 1, m - 1)
+                if s < NPOS:
+                    mm(s, m)
+            if s >= 1:
+                ep3(s - 1, MT - 1)
+
+        with tc.tile_pool(name="tmp", bufs=2) as tmp:
+            xraw = []
+            for m in range(MT):
+                xr = tmp.tile([P, E], BF16, name="xraw%d" % m, bufs=1)
+                xraw.append(xr)
+            for step in ["00","01","x0","x1","02","03","x2","x3","s","10","11","12","13"]:
+                if step[0] == "x":
+                    m = int(step[1])
+                    nc.sync.dma_start(out=xraw[m][:], in_=x[0, m * P:(m + 1) * P, :])
+                elif step[0] == "s":
+                    wqs = const.tile([P, PASSES, PACK], F32, name="wqs")
+                    nc.sync.dma_start(out=wqs[:], in_=w_q_scale.rearrange("(g p t) o -> p g (t o)", p=P, t=PACK))
                 else:
-                    byt = wqp.tile([P, PACK, NCH], U8, tag="wqb")
-                    nc.sync.dma_start(out=byt[:], in_=w_q_bytes[rows, cols].rearrange("(p t) n -> p t n", t=PACK))
-                    src = widep.tile([P, PACK, NCH], BF16, tag="wide")
-                    for t in range(PACK):
-                        nc.scalar.activation(out=src[:, t, :], in_=byt[:, t, :].bitcast(FP8), func=ACT.Copy,
-                                             scale=wqs[:, g, t:t + 1])
-                grouped = grp.tile([P, NCH, PACK], BF16, tag="grouped", align_bytes=64)
-                how = HOW[pos][g]
-                if FAST:
-                    gdst = grouped[:].rearrange("p (c i) t -> p c t i", i=4)
-                    gsrc = src[:].rearrange("p t (c i) -> p c t i", i=4)
-                else:
-                    gdst = grouped[:]
-                    gsrc = src[:].rearrange("p t c -> p c t")
-                if how == "S":
-                    nc.scalar.copy(out=gdst, in_=gsrc)
-                elif how == "V":
-                    nc.vector.tensor_copy(out=gdst, in_=gsrc)
-                elif how == "A":
-                    nc.any.tensor_copy(out=gdst, in_=gsrc)
-                else:
-                    gflat = grouped[:].rearrange("p c t -> p (c t)")
-                    for hb in range(2):
-                        pt = psum.tile([P, 1024], BF16, tag="pt", bufs=2)
-                        for q4 in range(2):
-                            c0 = hb * 256 + q4 * 128
-                            nc.tensor.matmul(out=pt[:, q4 * 512:(q4 + 1) * 512], lhsT=identb[:],
-                                             rhs=src[:, :, c0:c0 + 128].rearrange("p t c -> p c t"),
-                                             start=True, stop=True)
-                        nc.scalar.copy(out=gflat[:, hb * 1024:(hb + 1) * 1024], in_=pt[:])
-                codes = cdp.tile([P, NCH], U32, tag="codes", align_bytes=64)
-                scl = cdp.tile([P, NCH], U8, tag="scl", align_bytes=64)
-                nc.vector.quantize_mx(out=codes[:].bitcast(FP8X4), scales=scl[:],
-                                      in_=grouped[:].rearrange("p c t -> p (c t)"))
-                wc.append((codes, scl))
+                    load(int(step[0]), int(step[1]))
+
+            lnd = tmp.tile([P, PAIRS], F32, name="lnd", bufs=1)
+            nc.gpsimd.iota(lnd[:], pattern=[[1, PAIRS]], base=0, channel_multiplier=0,
+                           allow_small_or_imprecise_dtypes=True)
+            tpos = const.tile([P, MT], F32, name="tpos")
+            nc.gpsimd.iota(tpos[:], pattern=[[P, MT]], base=0, channel_multiplier=1,
+                           allow_small_or_imprecise_dtypes=True)
+            ident = const.tile([P, P], F32, name="ident")
+            make_identity(nc, ident[:])
+            identb = const.tile([P, P], BF16, name="identb")
+            make_identity(nc, identb[:])
+
+            nc.scalar.activation(out=lnd[:], in_=lnd[:], func=ACT.Ln, scale=2.0 / (1.4 * C), bias=0.4 * C / (1.4 * C))
+
+            freq = const.tile([P, PAIRS], F32, name="freq")
+            nc.vector.memset(freq[:, 0:1], 1.0)
+            tturn = const.tile([P, MT], F32, name="tturn")
+            t512 = const.tile([P, MT], F32, name="t512")
+            tneg = const.tile([P, MT], F32, name="tneg")
+            for lv in range(10):
+                w = 1 << lv
+                nc.vector.tensor_scalar(out=freq[:, w:2 * w], in0=freq[:, 0:w],
+                                        scalar1=pow(10000.0, -w / float(PAIRS)), scalar2=None, op0=ALU.mult)
+                if lv == 4:
+                    nc.vector.tensor_scalar(out=t512[:], in0=tpos[:], scalar1=1.0 / 512.0, scalar2=None, op0=ALU.mult)
+                if lv == 5:
+                    nc.vector.tensor_scalar(out=tturn[:], in0=tpos[:], scalar1=1.0 / (2.0 * math.pi), scalar2=None,
+                                            op0=ALU.mult)
+                if lv == 6:
+                    nc.vector.tensor_scalar(out=tneg[:], in0=tpos[:], scalar1=-1.0, scalar2=None, op0=ALU.mult)
+
+            ctab = []
+            stab = []
+            for m in range(MT):
+                ct = const.tile([P, PAIRS], F32, name="ctab%d" % m)
+                st = const.tile([P, 2, PAIRS], F32, name="stab%d" % m)
+                ctab.append(ct)
+                stab.append(st)
+                nc.scalar.activation(out=ct[:], in_=lnd[:], func=ACT.Exp, scale=t512[:, m:m + 1])
+
+            j0s = []
+            for m in range(MT):
+                tmax = m * P + P - 1
+                j0s.append(int(math.ceil(PAIRS * math.log(tmax / 3.14) / math.log(10000.0) / 32.0)) * 32)
+            nts = []
+            fracs = []
+            for mm_ in range(MT + 1):
+                if mm_ < MT:
+                    m = mm_
+                    nturn = tmp.tile([P, JRED], I32, tag="nturn")
+                    nc.vector.tensor_scalar(out=nturn[:, 0:j0s[m]], in0=freq[:, 0:j0s[m]], scalar1=tturn[:, m:m + 1],
+                                            scalar2=None, op0=ALU.mult)
+                    nts.append(nturn)
+                if mm_ >= 1:
+                    m = mm_ - 1
+                    frac = tmp.tile([P, JRED], F32, name="frac%d" % m, bufs=1)
+                    nc.vector.scalar_tensor_tensor(out=frac[:, 0:j0s[m]], in0=freq[:, 0:j0s[m]],
+                                                   scalar=tturn[:, m:m + 1], in1=nts[m][:, 0:j0s[m]],
+                                                   op0=ALU.mult, op1=ALU.subtract)
+                    fracs.append(frac)
+
+            xcodes = []
+            xscl = []
+            xgs = []
+
+            def x_turn(m):
+                words = xraw[m][:].bitcast(F32)
+                xg = tmp.tile([P, PASSES * P * PACK], BF16, name="xg%d" % m, bufs=1, align_bytes=64)
+                xgw = xg[:].bitcast(F32).rearrange("p (g r u) -> p g r u", g=PASSES, r=P, u=2)
+                for h in range(2):
+                    xt = psum.tile([P, 2, 2, P], F32, tag="acc")
+                    for gg in range(2):
+                        g = 2 * h + gg
+                        for u in range(2):
+                            nc.tensor.transpose(xt[:, gg, u, :], words[:, 256 * g + u:256 * (g + 1):2], ident[:])
+                    if XCOPY[2 * m + h] == "S":
+                        nc.scalar.copy(out=xgw[:, 2 * h:2 * h + 2], in_=xt[:].rearrange("p g u r -> p g r u"))
+                    else:
+                        nc.vector.tensor_copy(out=xgw[:, 2 * h:2 * h + 2], in_=xt[:].rearrange("p g u r -> p g r u"))
+                xgs.append(xg)
+
+            def x_quant(m):
+                xc = const.tile([P, PASSES * P], U32, name="xc%d" % m, align_bytes=64)
+                xs = const.tile([P, PASSES * P], U8, name="xs%d" % m, align_bytes=64)
+                nc.vector.quantize_mx(out=xc[:].bitcast(FP8X4), scales=xs[:], in_=xgs[m][:])
+                xcodes.append(xc)
+                xscl.append(xs)
+
+            cosvs = {}
+
+            def trig(m):
+                st = stab[m]
+                j0 = j0s[m]
+                frac = fracs[m]
+                cosv = st[:, 1, :]
+                nc.scalar.activation(out=st[:, 0, j0:], in_=freq[:, j0:], func=ACT.Sin, scale=tpos[:, m:m + 1])
+                nc.scalar.activation(out=cosv[:, j0:], in_=freq[:, j0:], func=ACT.Sin, scale=tneg[:, m:m + 1],
+                                     bias=0.5 * math.pi)
+                nc.scalar.activation(out=st[:, 0, 0:j0], in_=frac[:, 0:j0], func=ACT.Sin, scale=2.0 * math.pi)
+                afr = tmp.tile([P, JRED], F32, tag="afr")
+                nc.scalar.activation(out=afr[:, 0:j0], in_=frac[:, 0:j0], func=ACT.Abs)
+                nc.scalar.activation(out=cosv[:, 0:j0], in_=afr[:, 0:j0], func=ACT.Sin, scale=-2.0 * math.pi,
+                                     bias=0.5 * math.pi)
+                cosvs[m] = cosv
+
+            def table_mults(m):
+                ct, st = ctab[m], stab[m]
+                nc.vector.tensor_tensor(out=st[:, 0, :], in0=st[:, 0, :], in1=ct[:], op=ALU.mult)
+                nc.vector.tensor_tensor(out=ct[:], in0=st[:, 1, :], in1=ct[:], op=ALU.mult)
+                nc.vector.tensor_scalar(out=st[:, 1, :], in0=st[:, 0, :], scalar1=-1.0, scalar2=None, op0=ALU.mult)
 
             for m in range(MT):
-                acc = psum.tile([P, NCH], F32, tag="acc")
-                for g in range(PASSES):
-                    codes, scl = wc[g]
-                    nc.tensor.matmul_mx(out=acc[:],
-                                        lhsT=xcodes[m][:, g * P:(g + 1) * P].bitcast(FP8X4),
-                                        lhsT_scale=xscl[m][:, g * P:(g + 1) * P],
-                                        rhs=codes[:].bitcast(FP8X4), rhs_scale=scl[:],
-                                        start=(g == 0), stop=(g == PASSES - 1))
-                z = acc[:].rearrange("p (j e) -> p e j", e=2)
-                t1 = epp.tile([P, 2, JCH], F32, tag="t1")
-                nc.vector.tensor_tensor(out=t1[:], in0=z, in1=ctab[m][:, js].unsqueeze(1).to_broadcast([P, 2, JCH]),
-                                        op=ALU.mult)
-                t2 = epp.tile([P, 2, JCH], F32, tag="t2")
-                nc.vector.tensor_tensor(out=t2[:], in0=z, in1=stab[m][:, :, js], op=ALU.mult)
-                o = epp.tile([P, NCH], F32, tag="o")
-                adder = nc.gpsimd if ADD[pos][m] == "G" else nc.vector
-                adder.tensor_tensor(out=o[:].rearrange("p (j e) -> p j e", e=2),
-                                    in0=t1[:].rearrange("p e j -> p j e"),
-                                    in1=t2[:, ::-1, :].rearrange("p e j -> p j e"), op=ALU.add)
-                nc.sync.dma_start(out=dst[0, m * P:(m + 1) * P, cols], in_=o[:])
+                x_turn(m)
+            s_tasks(0)
+            HEAD = ["t0","t1","t2","t3","a0","m0","m1","s1","b0","m2","m3","a1"]
+            for step in HEAD:
+                if step[0] == "a":
+                    part_a(int(step[1]))
+                elif step[0] == "b":
+                    part_b(int(step[1]))
+                elif step[0] == "t":
+                    trig(int(step[1]))
+                elif step[0] == "s":
+                    s_tasks(int(step[1]))
+                elif step[0] == "m":
+                    table_mults(int(step[1]))
+
+        late["epp"] = ctx.enter_context(tc.tile_pool(name="epp", bufs=4))
+        for step in ["b1","a2","b2","a3","b3","a4","b4","a5","b5","a6","b6","a7","b7","b8"]:
+            if step[0] == "a":
+                part_a(int(step[1]))
+            else:
+                part_b(int(step[1]))

@@ -29,8 +29,8 @@ JCH = NCH // 2
 JRED = 576
 
 ORDER = ["k0","q0","k1","q1","k2","q2","k3","q3"]
-HOW = ["VVVV","PPVV","PPVS","PVSS","PPVS","PVSS","PPSS","PSSS"]
-ADD = ["GGGG","GGGG","GGGG","GGGG","GGGG","GGGG","GGGG","GGGV"]
+HOW = ["VVVV","PPVV","PPSS","PVSS","PPSS","PSSS","PPSS","PSSS"]
+ADD = ["GGDD","GGDD","GGDD","GGDD","GGDD","GGDD","GGGD","GVGV"]
 XCOPY = "SSSSSSSS"
 TM_AT = [[9,9],[9,9],[9,9],[9,9]]
 NPOS = len(ORDER)
@@ -174,6 +174,10 @@ def tile_multiscaleretention_pa_kernel(tc, x, w_q_bytes, w_q_scale, w_k, out_0, 
                 for g in range(PASSES):
                     if HOW[s][g] == "P":
                         pt_evac(s, g, "V")
+            if s >= 2:
+                for m in range(MT):
+                    if ADD[s - 2][m] == "D":
+                        ep3(s - 2, m)
             if s + 2 < NPOS:
                 load(s + 2, 0)
                 load(s + 2, 1)
@@ -200,11 +204,11 @@ def tile_multiscaleretention_pa_kernel(tc, x, w_q_bytes, w_q_scale, w_k, out_0, 
             for m in range(MT):
                 if s >= 1:
                     ep12(s - 1, m)
-                    if m >= 1:
+                    if m >= 1 and ADD[s - 1][m - 1] != "D":
                         ep3(s - 1, m - 1)
                 if s < NPOS:
                     mm(s, m)
-            if s >= 1:
+            if s >= 1 and ADD[s - 1][MT - 1] != "D":
                 ep3(s - 1, MT - 1)
 
         with tc.tile_pool(name="tmp", bufs=2) as tmp:
@@ -348,8 +352,8 @@ def tile_multiscaleretention_pa_kernel(tc, x, w_q_bytes, w_q_scale, w_k, out_0, 
                 elif step[0] == "m":
                     table_mults(int(step[1]))
 
-        late["epp"] = ctx.enter_context(tc.tile_pool(name="epp", bufs=4))
-        for step in ["b1","a2","b2","a3","b3","a4","b4","a5","b5","a6","b6","a7","b7","b8"]:
+        late["epp"] = ctx.enter_context(tc.tile_pool(name="epp", bufs=5))
+        for step in ["b1","a2","b2","a3","b3","a4","b4","a5","b5","a6","b6","a7","b7","a8","b8"]:
             if step[0] == "a":
                 part_a(int(step[1]))
             else:

@@ -29,8 +29,8 @@ JCH = NCH // 2
 JRED = 576
 
 ORDER = ["k0","q0","k1","q1","k2","q2","k3","q3"]
-HOW = ["VVVV","PPVV","PPSS","PVSS","PPSS","PSSS","PPSS","PSSS"]
-ADD = ["GGDD","GGDD","GGDD","GGDD","GGDD","GGDD","GGGD","GVGV"]
+HOW = ["VVVV","VVVV","VVSS","VVSS","VVSS","VSSS","VSSS","SSSS"]
+ADD = ["GGDD","GGDD","GGDD","GGDD","GGDD","GGDD","GGGG","GGVV"]
 XCOPY = "SSSSSSSS"
 TM_AT = [[9,9],[9,9],[9,9],[9,9]]
 NPOS = len(ORDER)
@@ -44,9 +44,9 @@ def tile_multiscaleretention_pa_kernel(tc, x, w_q_bytes, w_q_scale, w_k, out_0, 
         wkp = ctx.enter_context(tc.tile_pool(name="wkp", bufs=6))
         wqp = ctx.enter_context(tc.tile_pool(name="wqp", bufs=6))
         widep = ctx.enter_context(tc.tile_pool(name="widep", bufs=4))
-        grp = ctx.enter_context(tc.tile_pool(name="grp", bufs=6))
+        grp = ctx.enter_context(tc.tile_pool(name="grp", bufs=8))
         cdp = ctx.enter_context(tc.tile_pool(name="cdp", bufs=8))
-        psum = ctx.enter_context(tc.psum_pool(name="psum", bufs=4))
+        psum = ctx.enter_context(tc.psum_pool(name="psum", bufs=8))
         late = {}
 
         raw = {}
@@ -94,9 +94,11 @@ def tile_multiscaleretention_pa_kernel(tc, x, w_q_bytes, w_q_scale, w_k, out_0, 
         def inter(pos, g, eng):
             t = new_grouped(pos, g, eng)
             if eng == "S":
-                nc.scalar.copy(out=t[:], in_=wide[(pos, g)][:].rearrange("p t c -> p c t"))
+                nc.scalar.copy(out=t[:].rearrange("p (c i) t -> p c t i", i=4),
+                               in_=wide[(pos, g)][:].rearrange("p t (c i) -> p c t i", i=4))
             else:
-                nc.vector.tensor_copy(out=t[:], in_=wide[(pos, g)][:].rearrange("p t c -> p c t"))
+                nc.vector.tensor_copy(out=t[:].rearrange("p (c i) t -> p c t i", i=4),
+                                      in_=wide[(pos, g)][:].rearrange("p t (c i) -> p c t i", i=4))
 
         def pt_mm(pos, g):
             for hb in range(2):

@@ -22,18 +22,24 @@ P = 128
 PACK = 4
 K_PASS = P * PACK
 PASSES = E // K_PASS
-MT = T // P
+TILES = T // P
 NCH = 512
+CHUNKS = 2 * C // NCH
 PAIRS = C // 2
 JCH = NCH // 2
-JRED = 576
 
-ORDER = ["k0","q0","k1","q1","k2","q2","k3","q3"]
-HOW = ["VVVV","VVVV","VVSS","VVSS","VVSS","VSSS","VSSS","SSSS"]
-ADD = ["GGDD","GGDD","GGDD","GGDD","GGDD","GGDD","GGGG","GGVV"]
-XCOPY = "SSSSSSSS"
-TM_AT = [[9,9],[9,9],[9,9],[9,9]]
-NPOS = len(ORDER)
+VECTOR_UNITS = (4, 4, 2, 2, 2, 1, 1, 0)
+
+GPSIMD_TILES = 2
+
+PSUM_BANKS = 8
+
+RAW_BUFS = 6
+WIDE_BUFS = 4
+SCALAR_BUFS = 8
+VECTOR_BUFS = 3
+CODE_BUFS = 8
+XPOS_BUFS = 5
 
 
 def tile_multiscaleretention_pa_kernel(tc, x, w_q_bytes, w_q_scale, w_k, out_0, out_1):
@@ -41,322 +47,279 @@ def tile_multiscaleretention_pa_kernel(tc, x, w_q_bytes, w_q_scale, w_k, out_0, 
     with ExitStack() as ctx:
         ctx.enter_context(tc.manual_schedule(engines={ENG.DVE, ENG.Pool, ENG.Activation, ENG.PE}))
         const = ctx.enter_context(tc.tile_pool(name="const", bufs=1))
-        wkp = ctx.enter_context(tc.tile_pool(name="wkp", bufs=6))
-        wqp = ctx.enter_context(tc.tile_pool(name="wqp", bufs=6))
-        widep = ctx.enter_context(tc.tile_pool(name="widep", bufs=4))
-        grp = ctx.enter_context(tc.tile_pool(name="grp", bufs=8))
-        cdp = ctx.enter_context(tc.tile_pool(name="cdp", bufs=8))
-        psum = ctx.enter_context(tc.psum_pool(name="psum", bufs=8))
-        late = {}
+        rows_k = ctx.enter_context(tc.tile_pool(name="rows_k", bufs=RAW_BUFS))
+        rows_q = ctx.enter_context(tc.tile_pool(name="rows_q", bufs=RAW_BUFS))
+        widened = ctx.enter_context(tc.tile_pool(name="widened", bufs=WIDE_BUFS))
+        side_by_side = ctx.enter_context(tc.tile_pool(name="side_by_side", bufs=SCALAR_BUFS))
+        quantized = ctx.enter_context(tc.tile_pool(name="quantized", bufs=CODE_BUFS))
+        psum = ctx.enter_context(tc.psum_pool(name="psum", bufs=PSUM_BANKS))
 
-        raw = {}
-        wide = {}
+        byte_rows = {}
+        bf16_rows = {}
         grouped = {}
-        ptiles = {}
-        wcodes = {}
-        accs = {}
-        prods = {}
+        w_codes = {}
+        sums = {}
+        products = {}
+        xpos_tiles = []
 
-        def kind(pos):
-            return ORDER[pos][0]
+        def is_q(pos):
+            return pos % 2 == 1
 
-        def cols(pos):
-            c = int(ORDER[pos][1])
-            return slice(c * NCH, (c + 1) * NCH)
+        def channels(pos):
+            return slice((pos // 2) * NCH, (pos // 2 + 1) * NCH)
 
         def load(pos, g):
-            rows = slice(g * K_PASS, (g + 1) * K_PASS)
-            if kind(pos) == "k":
-                t = wkp.tile([P, PACK, NCH], BF16, tag="wk")
-                nc.sync.dma_start(out=t[:], in_=w_k[rows, cols(pos)].rearrange("(p t) n -> p t n", t=PACK))
-                wide[(pos, g)] = t
+            k_rows = slice(g * K_PASS, (g + 1) * K_PASS)
+            if is_q(pos):
+                unit_bytes = rows_q.tile([P, PACK, NCH], U8, tag="unit_bytes")
+                nc.sync.dma_start(out=unit_bytes[:],
+                                  in_=w_q_bytes[k_rows, channels(pos)].rearrange("(p t) n -> p t n", t=PACK))
+                byte_rows[(pos, g)] = unit_bytes
             else:
-                t = wqp.tile([P, PACK, NCH], U8, tag="wqb")
-                nc.sync.dma_start(out=t[:], in_=w_q_bytes[rows, cols(pos)].rearrange("(p t) n -> p t n", t=PACK))
-                raw[(pos, g)] = t
+                unit_rows = rows_k.tile([P, PACK, NCH], BF16, tag="unit_rows")
+                nc.sync.dma_start(out=unit_rows[:],
+                                  in_=w_k[k_rows, channels(pos)].rearrange("(p t) n -> p t n", t=PACK))
+                bf16_rows[(pos, g)] = unit_rows
 
         def widen(pos, g):
-            if kind(pos) == "q":
-                t = widep.tile([P, PACK, NCH], BF16, tag="wide")
-                for j in range(PACK):
-                    nc.scalar.activation(out=t[:, j, :], in_=raw[(pos, g)][:, j, :].bitcast(FP8), func=ACT.Copy,
-                                         scale=wqs[:, g, j:j + 1])
-                wide[(pos, g)] = t
+            unit_wide = widened.tile([P, PACK, NCH], BF16, tag="unit_wide")
+            for t in range(PACK):
+                nc.scalar.activation(out=unit_wide[:, t, :], in_=byte_rows[(pos, g)][:, t, :].bitcast(FP8),
+                                     func=ACT.Copy, scale=q_scale[:, g, t:t + 1])
+            bf16_rows[(pos, g)] = unit_wide
 
-        def new_grouped(pos, g, eng):
-            if eng == "S":
-                t = grp.tile([P, NCH, PACK], BF16, tag="gs", align_bytes=64)
+        def interleave(pos, g):
+            if g < VECTOR_UNITS[pos]:
+                unit_grouped = side_by_side.tile([P, NCH, PACK], BF16, tag="by_vector", align_bytes=64, bufs=VECTOR_BUFS)
+                copy = nc.vector.tensor_copy
             else:
-                t = grp.tile([P, NCH, PACK], BF16, tag="gv", align_bytes=64, bufs=3)
-            grouped[(pos, g)] = t
-            return t
+                unit_grouped = side_by_side.tile([P, NCH, PACK], BF16, tag="by_scalar", align_bytes=64)
+                copy = nc.scalar.copy
+            copy(out=unit_grouped[:].rearrange("p (c i) t -> p c t i", i=4),
+                 in_=bf16_rows[(pos, g)][:].rearrange("p t (c i) -> p c t i", i=4))
+            grouped[(pos, g)] = unit_grouped
 
-        def inter(pos, g, eng):
-            t = new_grouped(pos, g, eng)
-            if eng == "S":
-                nc.scalar.copy(out=t[:].rearrange("p (c i) t -> p c t i", i=4),
-                               in_=wide[(pos, g)][:].rearrange("p t (c i) -> p c t i", i=4))
-            else:
-                nc.vector.tensor_copy(out=t[:].rearrange("p (c i) t -> p c t i", i=4),
-                                      in_=wide[(pos, g)][:].rearrange("p t (c i) -> p c t i", i=4))
-
-        def pt_mm(pos, g):
-            for hb in range(2):
-                pt = psum.tile([P, 1024], BF16, tag="pt", bufs=4)
-                for q4 in range(2):
-                    c0 = hb * 256 + q4 * 128
-                    nc.tensor.matmul(out=pt[:, q4 * 512:(q4 + 1) * 512], lhsT=identb[:],
-                                     rhs=wide[(pos, g)][:, :, c0:c0 + 128].rearrange("p t c -> p c t"),
-                                     start=True, stop=True)
-                ptiles[(pos, g, hb)] = pt
-
-        def pt_evac(pos, g, eng):
-            t = new_grouped(pos, g, eng)
-            flat = t[:].rearrange("p c t -> p (c t)")
-            for hb in range(2):
-                if eng == "S":
-                    nc.scalar.copy(out=flat[:, hb * 1024:(hb + 1) * 1024], in_=ptiles[(pos, g, hb)][:])
-                else:
-                    nc.vector.tensor_copy(out=flat[:, hb * 1024:(hb + 1) * 1024], in_=ptiles[(pos, g, hb)][:])
-
-        def quant(pos, g):
-            codes = cdp.tile([P, NCH], U32, tag="codes", align_bytes=64)
-            scl = cdp.tile([P, NCH], U8, tag="scl", align_bytes=64)
-            nc.vector.quantize_mx(out=codes[:].bitcast(FP8X4), scales=scl[:],
+        def quantize(pos, g):
+            codes = quantized.tile([P, NCH], U32, tag="codes", align_bytes=64)
+            scales = quantized.tile([P, NCH], U8, tag="scales", align_bytes=64)
+            nc.vector.quantize_mx(out=codes[:].bitcast(FP8X4), scales=scales[:],
                                   in_=grouped[(pos, g)][:].rearrange("p c t -> p (c t)"))
-            wcodes[(pos, g)] = (codes, scl)
+            w_codes[(pos, g)] = (codes, scales)
 
-        def mm(pos, m):
-            acc = psum.tile([P, NCH], F32, tag="acc")
+        def multiply(pos, m):
+            bank = psum.tile([P, NCH], F32, tag="bank")
             for g in range(PASSES):
-                codes, scl = wcodes[(pos, g)]
-                nc.tensor.matmul_mx(out=acc[:],
-                                    lhsT=xcodes[m][:, g * P:(g + 1) * P].bitcast(FP8X4),
-                                    lhsT_scale=xscl[m][:, g * P:(g + 1) * P],
-                                    rhs=codes[:].bitcast(FP8X4), rhs_scale=scl[:],
+                codes, scales = w_codes[(pos, g)]
+                nc.tensor.matmul_mx(out=bank[:],
+                                    lhsT=x_codes[m][:, g * P:(g + 1) * P].bitcast(FP8X4),
+                                    lhsT_scale=x_scales[m][:, g * P:(g + 1) * P],
+                                    rhs=codes[:].bitcast(FP8X4), rhs_scale=scales[:],
                                     start=(g == 0), stop=(g == PASSES - 1))
-            accs[(pos, m)] = acc
+            sums[(pos, m)] = bank
 
-        def ep12(pos, m):
-            epp = late["epp"]
-            c = int(ORDER[pos][1])
-            js = slice(c * JCH, (c + 1) * JCH)
-            z = accs[(pos, m)][:].rearrange("p (j e) -> p e j", e=2)
-            t1 = epp.tile([P, 2, JCH], F32, tag="t1")
-            nc.vector.tensor_tensor(out=t1[:], in0=z, in1=ctab[m][:, js].unsqueeze(1).to_broadcast([P, 2, JCH]),
-                                    op=ALU.mult)
-            t2 = epp.tile([P, 2, JCH], F32, tag="t2")
-            nc.vector.tensor_tensor(out=t2[:], in0=z, in1=stab[m][:, :, js], op=ALU.mult)
-            prods[(pos, m)] = (t1, t2)
+        def make_products(pos, m):
+            pairs = slice((pos // 2) * JCH, (pos // 2 + 1) * JCH)
+            z = sums[(pos, m)][:].rearrange("p (j e) -> p e j", e=2)
+            pool = xpos_tiles[0]
+            by_cos = pool.tile([P, 2, JCH], F32, tag="by_cos")
+            nc.vector.tensor_tensor(out=by_cos[:], in0=z,
+                                    in1=cos_table[m][:, pairs].unsqueeze(1).to_broadcast([P, 2, JCH]), op=ALU.mult)
+            by_sin = pool.tile([P, 2, JCH], F32, tag="by_sin")
+            nc.vector.tensor_tensor(out=by_sin[:], in0=z, in1=sin_table[m][:, :, pairs], op=ALU.mult)
+            products[(pos, m)] = (by_cos, by_sin)
 
-        def ep3(pos, m):
-            epp = late["epp"]
-            t1, t2 = prods[(pos, m)]
-            dst = out_0 if kind(pos) == "q" else out_1
-            o = epp.tile([P, NCH], F32, tag="o")
-            adder = nc.gpsimd if ADD[pos][m] == "G" else nc.vector
-            adder.tensor_tensor(out=o[:].rearrange("p (j e) -> p j e", e=2),
-                                in0=t1[:].rearrange("p e j -> p j e"),
-                                in1=t2[:, ::-1, :].rearrange("p e j -> p j e"), op=ALU.add)
-            nc.sync.dma_start(out=dst[0, m * P:(m + 1) * P, cols(pos)], in_=o[:])
+        def add_and_store(pos, m):
+            by_cos, by_sin = products[(pos, m)]
+            pool = xpos_tiles[0]
+            rotated = pool.tile([P, NCH], F32, tag="rotated")
+            engine = nc.gpsimd if m < GPSIMD_TILES else nc.vector
+            engine.tensor_tensor(out=rotated[:].rearrange("p (j e) -> p j e", e=2),
+                                 in0=by_cos[:].rearrange("p e j -> p j e"),
+                                 in1=by_sin[:, ::-1, :].rearrange("p e j -> p j e"), op=ALU.add)
+            out = out_0 if is_q(pos) else out_1
+            nc.sync.dma_start(out=out[0, m * P:(m + 1) * P, channels(pos)], in_=rotated[:])
 
-        def s_tasks(pos):
-            for g in range(PASSES):
-                widen(pos, g)
-                if HOW[pos][g] in "PT":
-                    pt_mm(pos, g)
-            for g in range(PASSES):
-                if HOW[pos][g] == "T":
-                    pt_evac(pos, g, "S")
-                elif HOW[pos][g] == "S":
-                    inter(pos, g, "S")
-
-        def part_a(s):
-            if s < NPOS:
+        def scalar_prepares(pos):
+            if is_q(pos):
                 for g in range(PASSES):
-                    if HOW[s][g] == "P":
-                        pt_evac(s, g, "V")
-            if s >= 2:
-                for m in range(MT):
-                    if ADD[s - 2][m] == "D":
-                        ep3(s - 2, m)
-            if s + 2 < NPOS:
-                load(s + 2, 0)
-                load(s + 2, 1)
-            if 1 <= s and s + 1 < NPOS:
-                s_tasks(s + 1)
-            if s < NPOS:
-                ready = [g for g in range(PASSES) if HOW[s][g] in "ST"] + [g for g in range(PASSES) if HOW[s][g] == "P"]
-                for g in range(PASSES):
-                    if HOW[s][g] == "V":
-                        inter(s, g, "V")
-                        if ready:
-                            quant(s, ready.pop(0))
-                        ready.append(g)
-                if s + 2 < NPOS:
-                    load(s + 2, 2)
-                    load(s + 2, 3)
-                if s == 0:
-                    for m in range(MT):
-                        x_quant(m)
-                for g in ready:
-                    quant(s, g)
+                    widen(pos, g)
+            for g in range(VECTOR_UNITS[pos], PASSES):
+                interleave(pos, g)
 
-        def part_b(s):
-            for m in range(MT):
-                if s >= 1:
-                    ep12(s - 1, m)
-                    if m >= 1 and ADD[s - 1][m - 1] != "D":
-                        ep3(s - 1, m - 1)
-                if s < NPOS:
-                    mm(s, m)
-            if s >= 1 and ADD[s - 1][MT - 1] != "D":
-                ep3(s - 1, MT - 1)
+        def vector_adds(pos):
+            for m in range(GPSIMD_TILES, TILES):
+                add_and_store(pos, m)
 
-        with tc.tile_pool(name="tmp", bufs=2) as tmp:
-            xraw = []
-            for m in range(MT):
-                xr = tmp.tile([P, E], BF16, name="xraw%d" % m, bufs=1)
-                xraw.append(xr)
-            for step in ["00","01","x0","x1","02","03","x2","x3","s","10","11","12","13"]:
-                if step[0] == "x":
-                    m = int(step[1])
-                    nc.sync.dma_start(out=xraw[m][:], in_=x[0, m * P:(m + 1) * P, :])
-                elif step[0] == "s":
-                    wqs = const.tile([P, PASSES, PACK], F32, name="wqs")
-                    nc.sync.dma_start(out=wqs[:], in_=w_q_scale.rearrange("(g p t) o -> p g (t o)", p=P, t=PACK))
-                else:
-                    load(int(step[0]), int(step[1]))
+        def vector_prepares(pos):
+            waiting = list(range(VECTOR_UNITS[pos], PASSES))
+            for g in range(VECTOR_UNITS[pos]):
+                interleave(pos, g)
+                if waiting:
+                    quantize(pos, waiting.pop(0))
+                waiting.append(g)
+            return waiting
 
-            lnd = tmp.tile([P, PAIRS], F32, name="lnd", bufs=1)
-            nc.gpsimd.iota(lnd[:], pattern=[[1, PAIRS]], base=0, channel_multiplier=0,
+        def prepare(pos):
+            if pos + 2 < CHUNKS:
+                load(pos + 2, 0)
+                load(pos + 2, 1)
+            if 1 <= pos < CHUNKS - 1:
+                scalar_prepares(pos + 1)
+            waiting = vector_prepares(pos)
+            if pos + 2 < CHUNKS:
+                load(pos + 2, 2)
+                load(pos + 2, 3)
+            return waiting
+
+        def rotate(pos, then_multiply):
+            for m in range(TILES):
+                make_products(pos, m)
+                if 1 <= m <= GPSIMD_TILES:
+                    add_and_store(pos, m - 1)
+                if then_multiply:
+                    multiply(pos + 1, m)
+
+        with tc.tile_pool(name="head", bufs=2) as head:
+            x_rows = []
+            for m in range(TILES):
+                token_rows = head.tile([P, E], BF16, name="token_rows%d" % m, bufs=1)
+                x_rows.append(token_rows)
+            for half in range(2):
+                load(0, 2 * half)
+                load(0, 2 * half + 1)
+                for m in (2 * half, 2 * half + 1):
+                    nc.sync.dma_start(out=x_rows[m][:], in_=x[0, m * P:(m + 1) * P, :])
+            q_scale = const.tile([P, PASSES, PACK], F32, name="q_scale")
+            nc.sync.dma_start(out=q_scale[:], in_=w_q_scale.rearrange("(g p t) o -> p g (t o)", p=P, t=PACK))
+            for g in range(PASSES):
+                load(1, g)
+
+            ln_d = head.tile([P, PAIRS], F32, name="ln_d", bufs=1)
+            nc.gpsimd.iota(ln_d[:], pattern=[[1, PAIRS]], base=0, channel_multiplier=0,
                            allow_small_or_imprecise_dtypes=True)
-            tpos = const.tile([P, MT], F32, name="tpos")
-            nc.gpsimd.iota(tpos[:], pattern=[[P, MT]], base=0, channel_multiplier=1,
+            token = const.tile([P, TILES], F32, name="token")
+            nc.gpsimd.iota(token[:], pattern=[[P, TILES]], base=0, channel_multiplier=1,
                            allow_small_or_imprecise_dtypes=True)
-            ident = const.tile([P, P], F32, name="ident")
-            make_identity(nc, ident[:])
-            identb = const.tile([P, P], BF16, name="identb")
-            make_identity(nc, identb[:])
-
-            nc.scalar.activation(out=lnd[:], in_=lnd[:], func=ACT.Ln, scale=2.0 / (1.4 * C), bias=0.4 * C / (1.4 * C))
+            identity = const.tile([P, P], F32, name="identity")
+            make_identity(nc, identity[:])
+            nc.scalar.activation(out=ln_d[:], in_=ln_d[:], func=ACT.Ln, scale=2.0 / (1.4 * C), bias=0.4 * C / (1.4 * C))
 
             freq = const.tile([P, PAIRS], F32, name="freq")
             nc.vector.memset(freq[:, 0:1], 1.0)
-            tturn = const.tile([P, MT], F32, name="tturn")
-            t512 = const.tile([P, MT], F32, name="t512")
-            tneg = const.tile([P, MT], F32, name="tneg")
-            for lv in range(10):
-                w = 1 << lv
+            token_turns = const.tile([P, TILES], F32, name="token_turns")
+            token_512th = const.tile([P, TILES], F32, name="token_512th")
+            token_minus = const.tile([P, TILES], F32, name="token_minus")
+            per_token = {4: (token_512th, 1.0 / 512.0), 5: (token_turns, 1.0 / (2.0 * math.pi)), 6: (token_minus, -1.0)}
+            for level in range(10):
+                w = 1 << level
                 nc.vector.tensor_scalar(out=freq[:, w:2 * w], in0=freq[:, 0:w],
                                         scalar1=pow(10000.0, -w / float(PAIRS)), scalar2=None, op0=ALU.mult)
-                if lv == 4:
-                    nc.vector.tensor_scalar(out=t512[:], in0=tpos[:], scalar1=1.0 / 512.0, scalar2=None, op0=ALU.mult)
-                if lv == 5:
-                    nc.vector.tensor_scalar(out=tturn[:], in0=tpos[:], scalar1=1.0 / (2.0 * math.pi), scalar2=None,
-                                            op0=ALU.mult)
-                if lv == 6:
-                    nc.vector.tensor_scalar(out=tneg[:], in0=tpos[:], scalar1=-1.0, scalar2=None, op0=ALU.mult)
-
-            ctab = []
-            stab = []
-            for m in range(MT):
-                ct = const.tile([P, PAIRS], F32, name="ctab%d" % m)
-                st = const.tile([P, 2, PAIRS], F32, name="stab%d" % m)
-                ctab.append(ct)
-                stab.append(st)
-                nc.scalar.activation(out=ct[:], in_=lnd[:], func=ACT.Exp, scale=t512[:, m:m + 1])
-
-            j0s = []
-            for m in range(MT):
-                tmax = m * P + P - 1
-                j0s.append(int(math.ceil(PAIRS * math.log(tmax / 3.14) / math.log(10000.0) / 32.0)) * 32)
-            nts = []
-            fracs = []
-            for mm_ in range(MT + 1):
-                if mm_ < MT:
-                    m = mm_
-                    nturn = tmp.tile([P, JRED], I32, tag="nturn")
-                    nc.vector.tensor_scalar(out=nturn[:, 0:j0s[m]], in0=freq[:, 0:j0s[m]], scalar1=tturn[:, m:m + 1],
+                if level in per_token:
+                    nc.vector.tensor_scalar(out=per_token[level][0][:], in0=token[:], scalar1=per_token[level][1],
                                             scalar2=None, op0=ALU.mult)
-                    nts.append(nturn)
-                if mm_ >= 1:
-                    m = mm_ - 1
-                    frac = tmp.tile([P, JRED], F32, name="frac%d" % m, bufs=1)
-                    nc.vector.scalar_tensor_tensor(out=frac[:, 0:j0s[m]], in0=freq[:, 0:j0s[m]],
-                                                   scalar=tturn[:, m:m + 1], in1=nts[m][:, 0:j0s[m]],
+
+            cos_table = []
+            sin_table = []
+            for m in range(TILES):
+                table_c = const.tile([P, PAIRS], F32, name="cos_table%d" % m)
+                table_s = const.tile([P, 2, PAIRS], F32, name="sin_table%d" % m)
+                cos_table.append(table_c)
+                sin_table.append(table_s)
+                nc.scalar.activation(out=table_c[:], in_=ln_d[:], func=ACT.Exp, scale=token_512th[:, m:m + 1])
+
+            small = []
+            for m in range(TILES):
+                small.append(32 * int(math.ceil(PAIRS * math.log((m * P + P - 1) / 3.14) / math.log(10000.0) / 32.0)))
+            reduced = max(small)
+            wholes = []
+            parts = []
+            for step in range(TILES + 1):
+                if step < TILES:
+                    m = step
+                    whole = head.tile([P, reduced], I32, tag="whole")
+                    nc.vector.tensor_scalar(out=whole[:, 0:small[m]], in0=freq[:, 0:small[m]],
+                                            scalar1=token_turns[:, m:m + 1], scalar2=None, op0=ALU.mult)
+                    wholes.append(whole)
+                if step >= 1:
+                    m = step - 1
+                    part = head.tile([P, reduced], F32, name="part%d" % m, bufs=1)
+                    nc.vector.scalar_tensor_tensor(out=part[:, 0:small[m]], in0=freq[:, 0:small[m]],
+                                                   scalar=token_turns[:, m:m + 1], in1=wholes[m][:, 0:small[m]],
                                                    op0=ALU.mult, op1=ALU.subtract)
-                    fracs.append(frac)
+                    parts.append(part)
 
-            xcodes = []
-            xscl = []
-            xgs = []
-
-            def x_turn(m):
-                words = xraw[m][:].bitcast(F32)
-                xg = tmp.tile([P, PASSES * P * PACK], BF16, name="xg%d" % m, bufs=1, align_bytes=64)
-                xgw = xg[:].bitcast(F32).rearrange("p (g r u) -> p g r u", g=PASSES, r=P, u=2)
-                for h in range(2):
-                    xt = psum.tile([P, 2, 2, P], F32, tag="acc")
+            x_grouped = []
+            for m in range(TILES):
+                words = x_rows[m][:].bitcast(F32)
+                tile_grouped = head.tile([P, PASSES * P * PACK], BF16, name="x_grouped%d" % m, bufs=1, align_bytes=64)
+                as_words = tile_grouped[:].bitcast(F32).rearrange("p (g r u) -> p g r u", g=PASSES, r=P, u=2)
+                for half in range(2):
+                    turned = psum.tile([P, 2, 2, P], F32, tag="bank")
                     for gg in range(2):
-                        g = 2 * h + gg
+                        g = 2 * half + gg
                         for u in range(2):
-                            nc.tensor.transpose(xt[:, gg, u, :], words[:, 256 * g + u:256 * (g + 1):2], ident[:])
-                    if XCOPY[2 * m + h] == "S":
-                        nc.scalar.copy(out=xgw[:, 2 * h:2 * h + 2], in_=xt[:].rearrange("p g u r -> p g r u"))
-                    else:
-                        nc.vector.tensor_copy(out=xgw[:, 2 * h:2 * h + 2], in_=xt[:].rearrange("p g u r -> p g r u"))
-                xgs.append(xg)
+                            nc.tensor.transpose(turned[:, gg, u, :], words[:, 256 * g + u:256 * (g + 1):2], identity[:])
+                    nc.scalar.copy(out=as_words[:, 2 * half:2 * half + 2], in_=turned[:].rearrange("p g u r -> p g r u"))
+                x_grouped.append(tile_grouped)
 
-            def x_quant(m):
-                xc = const.tile([P, PASSES * P], U32, name="xc%d" % m, align_bytes=64)
-                xs = const.tile([P, PASSES * P], U8, name="xs%d" % m, align_bytes=64)
-                nc.vector.quantize_mx(out=xc[:].bitcast(FP8X4), scales=xs[:], in_=xgs[m][:])
-                xcodes.append(xc)
-                xscl.append(xs)
-
-            cosvs = {}
-
-            def trig(m):
-                st = stab[m]
-                j0 = j0s[m]
-                frac = fracs[m]
-                cosv = st[:, 1, :]
-                nc.scalar.activation(out=st[:, 0, j0:], in_=freq[:, j0:], func=ACT.Sin, scale=tpos[:, m:m + 1])
-                nc.scalar.activation(out=cosv[:, j0:], in_=freq[:, j0:], func=ACT.Sin, scale=tneg[:, m:m + 1],
+            def sines(m):
+                s = small[m]
+                sin_a = sin_table[m][:, 0, :]
+                cos_a = sin_table[m][:, 1, :]
+                nc.scalar.activation(out=sin_a[:, s:], in_=freq[:, s:], func=ACT.Sin, scale=token[:, m:m + 1])
+                nc.scalar.activation(out=cos_a[:, s:], in_=freq[:, s:], func=ACT.Sin, scale=token_minus[:, m:m + 1],
                                      bias=0.5 * math.pi)
-                nc.scalar.activation(out=st[:, 0, 0:j0], in_=frac[:, 0:j0], func=ACT.Sin, scale=2.0 * math.pi)
-                afr = tmp.tile([P, JRED], F32, tag="afr")
-                nc.scalar.activation(out=afr[:, 0:j0], in_=frac[:, 0:j0], func=ACT.Abs)
-                nc.scalar.activation(out=cosv[:, 0:j0], in_=afr[:, 0:j0], func=ACT.Sin, scale=-2.0 * math.pi,
+                nc.scalar.activation(out=sin_a[:, 0:s], in_=parts[m][:, 0:s], func=ACT.Sin, scale=2.0 * math.pi)
+                size = head.tile([P, reduced], F32, tag="size")
+                nc.scalar.activation(out=size[:, 0:s], in_=parts[m][:, 0:s], func=ACT.Abs)
+                nc.scalar.activation(out=cos_a[:, 0:s], in_=size[:, 0:s], func=ACT.Sin, scale=-2.0 * math.pi,
                                      bias=0.5 * math.pi)
-                cosvs[m] = cosv
 
-            def table_mults(m):
-                ct, st = ctab[m], stab[m]
-                nc.vector.tensor_tensor(out=st[:, 0, :], in0=st[:, 0, :], in1=ct[:], op=ALU.mult)
-                nc.vector.tensor_tensor(out=ct[:], in0=st[:, 1, :], in1=ct[:], op=ALU.mult)
-                nc.vector.tensor_scalar(out=st[:, 1, :], in0=st[:, 0, :], scalar1=-1.0, scalar2=None, op0=ALU.mult)
+            def finish_tables(m):
+                table_c, table_s = cos_table[m], sin_table[m]
+                nc.vector.tensor_tensor(out=table_s[:, 0, :], in0=table_s[:, 0, :], in1=table_c[:], op=ALU.mult)
+                nc.vector.tensor_tensor(out=table_c[:], in0=table_s[:, 1, :], in1=table_c[:], op=ALU.mult)
+                nc.vector.tensor_scalar(out=table_s[:, 1, :], in0=table_s[:, 0, :], scalar1=-1.0, scalar2=None,
+                                        op0=ALU.mult)
 
-            for m in range(MT):
-                x_turn(m)
-            s_tasks(0)
-            HEAD = ["t0","t1","t2","t3","a0","m0","m1","s1","b0","m2","m3","a1"]
-            for step in HEAD:
-                if step[0] == "a":
-                    part_a(int(step[1]))
-                elif step[0] == "b":
-                    part_b(int(step[1]))
-                elif step[0] == "t":
-                    trig(int(step[1]))
-                elif step[0] == "s":
-                    s_tasks(int(step[1]))
-                elif step[0] == "m":
-                    table_mults(int(step[1]))
+            for m in range(TILES):
+                sines(m)
 
-        late["epp"] = ctx.enter_context(tc.tile_pool(name="epp", bufs=5))
-        for step in ["b1","a2","b2","a3","b3","a4","b4","a5","b5","a6","b6","a7","b7","a8","b8"]:
-            if step[0] == "a":
-                part_a(int(step[1]))
-            else:
-                part_b(int(step[1]))
+            waiting = prepare(0)
+            x_codes = []
+            x_scales = []
+            for m in range(TILES):
+                tile_codes = const.tile([P, PASSES * P], U32, name="x_codes%d" % m, align_bytes=64)
+                tile_scales = const.tile([P, PASSES * P], U8, name="x_scales%d" % m, align_bytes=64)
+                nc.vector.quantize_mx(out=tile_codes[:].bitcast(FP8X4), scales=tile_scales[:], in_=x_grouped[m][:])
+                x_codes.append(tile_codes)
+                x_scales.append(tile_scales)
+            for g in waiting:
+                quantize(0, g)
+            finish_tables(0)
+            finish_tables(1)
+            scalar_prepares(1)
+            for m in range(TILES):
+                multiply(0, m)
+            finish_tables(2)
+            finish_tables(3)
+            for g in prepare(1):
+                quantize(1, g)
+
+        xpos_tiles.append(ctx.enter_context(tc.tile_pool(name="xpos_tiles", bufs=XPOS_BUFS)))
+        rotate(0, True)
+        for pos in range(2, CHUNKS - 1):
+            vector_adds(pos - 2)
+            for g in prepare(pos):
+                quantize(pos, g)
+            rotate(pos - 1, True)
+        last = CHUNKS - 1
+        vector_adds(last - 2)
+        rotate(last - 1, False)
+        for g in prepare(last):
+            quantize(last, g)
+        for m in range(TILES):
+            multiply(last, m)
+        vector_adds(last - 1)
+        rotate(last, False)
+        vector_adds(last)

@@ -119,13 +119,14 @@ def tile_multiscaleretention_pa_kernel(tc, x, w_q_bytes, w_q_scale, w_k, out_0, 
 
         def make_products(pos, m):
             pairs = slice((pos // 2) * JCH, (pos // 2 + 1) * JCH)
-            z = sums[(pos, m)][:].rearrange("p (j e) -> p e j", e=2)
+            z = sums[(pos, m)][:].rearrange("p (j e) -> p j e", e=2)
             pool = xpos_tiles[0]
-            by_cos = pool.tile([P, 2, JCH], F32, tag="by_cos")
+            by_cos = pool.tile([P, JCH, 2], F32, tag="by_cos")
             nc.vector.tensor_tensor(out=by_cos[:], in0=z,
-                                    in1=cos_table[m][:, pairs].unsqueeze(1).to_broadcast([P, 2, JCH]), op=ALU.mult)
-            by_sin = pool.tile([P, 2, JCH], F32, tag="by_sin")
-            nc.vector.tensor_tensor(out=by_sin[:], in0=z, in1=sin_table[m][:, :, pairs], op=ALU.mult)
+                                    in1=cos_table[m][:, pairs].unsqueeze(2).to_broadcast([P, JCH, 2]), op=ALU.mult)
+            by_sin = pool.tile([P, JCH, 2], F32, tag="by_sin")
+            nc.vector.tensor_tensor(out=by_sin[:], in0=z[:, :, ::-1],
+                                    in1=sin_table[m][:, :, pairs].rearrange("p e j -> p j e"), op=ALU.mult)
             products[(pos, m)] = (by_cos, by_sin)
 
         def add_and_store(pos, m):
@@ -133,9 +134,8 @@ def tile_multiscaleretention_pa_kernel(tc, x, w_q_bytes, w_q_scale, w_k, out_0, 
             pool = xpos_tiles[0]
             rotated = pool.tile([P, NCH], F32, tag="rotated")
             engine = nc.gpsimd if m < GPSIMD_TILES else nc.vector
-            engine.tensor_tensor(out=rotated[:].rearrange("p (j e) -> p j e", e=2),
-                                 in0=by_cos[:].rearrange("p e j -> p j e"),
-                                 in1=by_sin[:, ::-1, :].rearrange("p e j -> p j e"), op=ALU.add)
+            engine.tensor_tensor(out=rotated[:], in0=by_cos[:].rearrange("p j e -> p (j e)"),
+                                 in1=by_sin[:].rearrange("p j e -> p (j e)"), op=ALU.add)
             out = out_0 if is_q(pos) else out_1
             nc.sync.dma_start(out=out[0, m * P:(m + 1) * P, channels(pos)], in_=rotated[:])
 
@@ -264,8 +264,8 @@ def tile_multiscaleretention_pa_kernel(tc, x, w_q_bytes, w_q_scale, w_k, out_0, 
 
             def sines(m):
                 s = small[m]
-                sin_a = sin_table[m][:, 0, :]
-                cos_a = sin_table[m][:, 1, :]
+                sin_a = sin_table[m][:, 1, :]
+                cos_a = sin_table[m][:, 0, :]
                 nc.scalar.activation(out=sin_a[:, s:], in_=freq[:, s:], func=ACT.Sin, scale=token[:, m:m + 1])
                 nc.scalar.activation(out=cos_a[:, s:], in_=freq[:, s:], func=ACT.Sin, scale=token_minus[:, m:m + 1],
                                      bias=0.5 * math.pi)
@@ -277,9 +277,9 @@ def tile_multiscaleretention_pa_kernel(tc, x, w_q_bytes, w_q_scale, w_k, out_0, 
 
             def finish_tables(m):
                 table_c, table_s = cos_table[m], sin_table[m]
-                nc.vector.tensor_tensor(out=table_s[:, 0, :], in0=table_s[:, 0, :], in1=table_c[:], op=ALU.mult)
-                nc.vector.tensor_tensor(out=table_c[:], in0=table_s[:, 1, :], in1=table_c[:], op=ALU.mult)
-                nc.vector.tensor_scalar(out=table_s[:, 1, :], in0=table_s[:, 0, :], scalar1=-1.0, scalar2=None,
+                nc.vector.tensor_tensor(out=table_s[:, 1, :], in0=table_s[:, 1, :], in1=table_c[:], op=ALU.mult)
+                nc.vector.tensor_tensor(out=table_c[:], in0=table_s[:, 0, :], in1=table_c[:], op=ALU.mult)
+                nc.vector.tensor_scalar(out=table_s[:, 0, :], in0=table_s[:, 1, :], scalar1=-1.0, scalar2=None,
                                         op0=ALU.mult)
 
             for m in range(TILES):

@@ -30,7 +30,7 @@ JCH = NCH // 2
 
 VECTOR_UNITS = (4, 4, 2, 2, 2, 1, 1, 0)
 
-GPSIMD_TILES = 2
+GPSIMD_TILES = 3
 
 PSUM_BANKS = 8
 

@@ -28,11 +28,14 @@ CHUNKS = 2 * C // NCH
 PAIRS = C // 2
 JCH = NCH // 2
 
-VECTOR_UNITS = (4, 4, 2, 2, 2, 1, 1, 0)
+VECTOR_UNITS = (4, 4, 1, 1, 1, 1, 0, 0)
+
+TENSOR_UNITS = (0, 0, 2, 2, 2, 2, 2, 2)
 
 GPSIMD_TILES = 3
 
-PSUM_BANKS = 8
+SUM_BANKS = 4
+THROUGH_BANKS = 4
 
 RAW_BUFS = 6
 WIDE_BUFS = 4
@@ -52,11 +55,12 @@ def tile_multiscaleretention_pa_kernel(tc, x, w_q_bytes, w_q_scale, w_k, out_0, 
         widened = ctx.enter_context(tc.tile_pool(name="widened", bufs=WIDE_BUFS))
         side_by_side = ctx.enter_context(tc.tile_pool(name="side_by_side", bufs=SCALAR_BUFS))
         quantized = ctx.enter_context(tc.tile_pool(name="quantized", bufs=CODE_BUFS))
-        psum = ctx.enter_context(tc.psum_pool(name="psum", bufs=PSUM_BANKS))
+        psum = ctx.enter_context(tc.psum_pool(name="psum", bufs=SUM_BANKS))
 
         byte_rows = {}
         bf16_rows = {}
         grouped = {}
+        passed = {}
         w_codes = {}
         sums = {}
         products = {}
@@ -99,6 +103,25 @@ def tile_multiscaleretention_pa_kernel(tc, x, w_q_bytes, w_q_scale, w_k, out_0, 
                  in_=bf16_rows[(pos, g)][:].rearrange("p t (c i) -> p c t i", i=4))
             grouped[(pos, g)] = unit_grouped
 
+        def pass_through(pos, g):
+            banks = []
+            for half in range(2):
+                bank = psum.tile([P, 2 * NCH], BF16, tag="through", bufs=THROUGH_BANKS)
+                for quarter in range(2):
+                    c0 = (2 * half + quarter) * P
+                    nc.tensor.matmul(out=bank[:, quarter * NCH:(quarter + 1) * NCH], lhsT=identity_bf16[:],
+                                     rhs=bf16_rows[(pos, g)][:, :, c0:c0 + P].rearrange("p t c -> p c t"),
+                                     start=True, stop=True)
+                banks.append(bank)
+            passed[(pos, g)] = banks
+
+        def empty_through(pos, g):
+            unit_grouped = side_by_side.tile([P, NCH, PACK], BF16, tag="by_scalar", align_bytes=64)
+            flat = unit_grouped[:].rearrange("p c t -> p (c t)")
+            for half in range(2):
+                nc.scalar.copy(out=flat[:, half * 2 * NCH:(half + 1) * 2 * NCH], in_=passed[(pos, g)][half][:])
+            grouped[(pos, g)] = unit_grouped
+
         def quantize(pos, g):
             codes = quantized.tile([P, NCH], U32, tag="codes", align_bytes=64)
             scales = quantized.tile([P, NCH], U8, tag="scales", align_bytes=64)
@@ -107,7 +130,7 @@ def tile_multiscaleretention_pa_kernel(tc, x, w_q_bytes, w_q_scale, w_k, out_0, 
             w_codes[(pos, g)] = (codes, scales)
 
         def multiply(pos, m):
-            bank = psum.tile([P, NCH], F32, tag="bank")
+            bank = psum.tile([P, NCH], F32, tag="bank", bufs=SUM_BANKS)
             for g in range(PASSES):
                 codes, scales = w_codes[(pos, g)]
                 nc.tensor.matmul_mx(out=bank[:],
@@ -140,18 +163,30 @@ def tile_multiscaleretention_pa_kernel(tc, x, w_q_bytes, w_q_scale, w_k, out_0, 
             nc.sync.dma_start(out=out[0, m * P:(m + 1) * P, channels(pos)], in_=rotated[:])
 
         def scalar_prepares(pos):
+            first = VECTOR_UNITS[pos]
+            by_tensor = list(range(first, first + TENSOR_UNITS[pos]))
+            by_scalar = list(range(first + TENSOR_UNITS[pos], PASSES))
             if is_q(pos):
-                for g in range(PASSES):
+                for g in by_tensor:
                     widen(pos, g)
-            for g in range(VECTOR_UNITS[pos], PASSES):
+                    pass_through(pos, g)
+                for g in by_scalar + list(range(first)):
+                    widen(pos, g)
+            else:
+                for g in by_tensor:
+                    pass_through(pos, g)
+            for g in by_scalar:
                 interleave(pos, g)
+            for g in by_tensor:
+                empty_through(pos, g)
 
         def vector_adds(pos):
             for m in range(GPSIMD_TILES, TILES):
                 add_and_store(pos, m)
 
         def vector_prepares(pos):
-            waiting = list(range(VECTOR_UNITS[pos], PASSES))
+            first = VECTOR_UNITS[pos]
+            waiting = list(range(first + TENSOR_UNITS[pos], PASSES)) + list(range(first, first + TENSOR_UNITS[pos]))
             for g in range(VECTOR_UNITS[pos]):
                 interleave(pos, g)
                 if waiting:
@@ -202,6 +237,8 @@ def tile_multiscaleretention_pa_kernel(tc, x, w_q_bytes, w_q_scale, w_k, out_0, 
                            allow_small_or_imprecise_dtypes=True)
             identity = const.tile([P, P], F32, name="identity")
             make_identity(nc, identity[:])
+            identity_bf16 = const.tile([P, P], BF16, name="identity_bf16")
+            make_identity(nc, identity_bf16[:])
             nc.scalar.activation(out=ln_d[:], in_=ln_d[:], func=ACT.Ln, scale=2.0 / (1.4 * C), bias=0.4 * C / (1.4 * C))
 
             freq = const.tile([P, PAIRS], F32, name="freq")
@@ -254,7 +291,10 @@ def tile_multiscaleretention_pa_kernel(tc, x, w_q_bytes, w_q_scale, w_k, out_0, 
                 tile_grouped = head.tile([P, PASSES * P * PACK], BF16, name="x_grouped%d" % m, bufs=1, align_bytes=64)
                 as_words = tile_grouped[:].bitcast(F32).rearrange("p (g r u) -> p g r u", g=PASSES, r=P, u=2)
                 for half in range(2):
-                    turned = psum.tile([P, 2, 2, P], F32, tag="bank")
+                    if half == 0:
+                        turned = psum.tile([P, 2, 2, P], F32, tag="bank", bufs=SUM_BANKS)
+                    else:
+                        turned = psum.tile([P, 2, 2, P], F32, tag="through", bufs=THROUGH_BANKS)
                     for gg in range(2):
                         g = 2 * half + gg
                         for u in range(2):

@@ -28,11 +28,11 @@ CHUNKS = 2 * C // NCH
 PAIRS = C // 2
 JCH = NCH // 2
 
-VECTOR_UNITS = (4, 4, 1, 1, 1, 1, 0, 0)
+VECTOR_UNITS = (4, 4, 1, 1, 1, 1, 1, 0)
 
-TENSOR_UNITS = (0, 0, 2, 2, 2, 2, 2, 2)
+TENSOR_UNITS = (0, 0, 1, 2, 1, 2, 1, 2)
 
-GPSIMD_TILES = 3
+GPSIMD_TILES = 2
 
 SUM_BANKS = 4
 THROUGH_BANKS = 4

@@ -28,11 +28,12 @@ CHUNKS = 2 * C // NCH
 PAIRS = C // 2
 JCH = NCH // 2
 
-VECTOR_UNITS = (4, 4, 1, 1, 1, 1, 1, 0)
+VECTOR_UNITS = (4, 4, 2, 1, 1, 1, 1, 0)
 
 TENSOR_UNITS = (0, 0, 1, 2, 1, 2, 1, 2)
 
 GPSIMD_TILES = 2
+LATE_TILE = 2
 
 SUM_BANKS = 4
 THROUGH_BANKS = 4
@@ -42,7 +43,7 @@ WIDE_BUFS = 4
 SCALAR_BUFS = 8
 VECTOR_BUFS = 3
 CODE_BUFS = 8
-XPOS_BUFS = 5
+XPOS_BUFS = 6
 
 
 def tile_multiscaleretention_pa_kernel(tc, x, w_q_bytes, w_q_scale, w_k, out_0, out_1):
@@ -156,7 +157,7 @@ def tile_multiscaleretention_pa_kernel(tc, x, w_q_bytes, w_q_scale, w_k, out_0, 
             by_cos, by_sin = products[(pos, m)]
             pool = xpos_tiles[0]
             rotated = pool.tile([P, NCH], F32, tag="rotated")
-            engine = nc.gpsimd if m < GPSIMD_TILES else nc.vector
+            engine = nc.gpsimd if m < GPSIMD_TILES or (m == LATE_TILE and pos < CHUNKS - 1) else nc.vector
             engine.tensor_tensor(out=rotated[:], in0=by_cos[:].rearrange("p j e -> p (j e)"),
                                  in1=by_sin[:].rearrange("p j e -> p (j e)"), op=ALU.add)
             out = out_0 if is_q(pos) else out_1
@@ -182,7 +183,8 @@ def tile_multiscaleretention_pa_kernel(tc, x, w_q_bytes, w_q_scale, w_k, out_0, 
 
         def vector_adds(pos):
             for m in range(GPSIMD_TILES, TILES):
-                add_and_store(pos, m)
+                if m != LATE_TILE or pos == CHUNKS - 1:
+                    add_and_store(pos, m)
 
         def vector_prepares(pos):
             first = VECTOR_UNITS[pos]
@@ -207,6 +209,10 @@ def tile_multiscaleretention_pa_kernel(tc, x, w_q_bytes, w_q_scale, w_k, out_0, 
             return waiting
 
         def rotate(pos, then_multiply):
+            if pos >= 1:
+                late = products[(pos - 1, LATE_TILE)][1]
+                nc.vector.tensor_copy(out=late[:, 0:1, :], in_=late[:, 0:1, :])
+                add_and_store(pos - 1, LATE_TILE)
             for m in range(TILES):
                 make_products(pos, m)
                 if 1 <= m <= GPSIMD_TILES:

@@ -28,9 +28,9 @@ CHUNKS = 2 * C // NCH
 PAIRS = C // 2
 JCH = NCH // 2
 
-VECTOR_UNITS = (4, 4, 2, 1, 1, 1, 1, 0)
+VECTOR_UNITS = (4, 4, 1, 1, 1, 1, 0, 0)
 
-TENSOR_UNITS = (0, 0, 1, 2, 1, 2, 1, 2)
+TENSOR_UNITS = (0, 0, 2, 2, 2, 2, 2, 2)
 
 GPSIMD_TILES = 2
 LATE_TILE = 2
@@ -110,8 +110,8 @@ def tile_multiscaleretention_pa_kernel(tc, x, w_q_bytes, w_q_scale, w_k, out_0, 
                 bank = psum.tile([P, 2 * NCH], BF16, tag="through", bufs=THROUGH_BANKS)
                 for quarter in range(2):
                     c0 = (2 * half + quarter) * P
-                    nc.tensor.matmul(out=bank[:, quarter * NCH:(quarter + 1) * NCH], lhsT=identity_bf16[:],
-                                     rhs=bf16_rows[(pos, g)][:, :, c0:c0 + P].rearrange("p t c -> p c t"),
+                    nc.tensor.matmul(out=bank[:, quarter * NCH:(quarter + 1) * NCH].rearrange("p (c t) -> p t c", t=PACK),
+                                     lhsT=identity_bf16[:], rhs=bf16_rows[(pos, g)][:, :, c0:c0 + P],
                                      start=True, stop=True)
                 banks.append(bank)
             passed[(pos, g)] = banks

@@ -28,11 +28,12 @@ CHUNKS = 2 * C // NCH
 PAIRS = C // 2
 JCH = NCH // 2
 
-VECTOR_UNITS = (4, 4, 1, 1, 1, 1, 0, 0)
+VECTOR_UNITS = (4, 4, 1, 1, 1, 1, 1, 0)
 
-TENSOR_UNITS = (0, 0, 2, 2, 2, 2, 2, 2)
+TENSOR_UNITS = (0, 0, 2, 2, 1, 2, 1, 2)
 
 GPSIMD_TILES = 2
+WIDENED_BY_VECTOR = 0
 LATE_TILE = 2
 
 SUM_BANKS = 4
@@ -89,12 +90,21 @@ def tile_multiscaleretention_pa_kernel(tc, x, w_q_bytes, w_q_scale, w_k, out_0, 
         def widen(pos, g):
             unit_wide = widened.tile([P, PACK, NCH], BF16, tag="unit_wide")
             for t in range(PACK):
-                nc.scalar.activation(out=unit_wide[:, t, :], in_=byte_rows[(pos, g)][:, t, :].bitcast(FP8),
-                                     func=ACT.Copy, scale=q_scale[:, g, t:t + 1])
+                if pos == 1 and g >= PASSES - WIDENED_BY_VECTOR:
+                    nc.vector.tensor_scalar(out=unit_wide[:, t, :], in0=byte_rows[(pos, g)][:, t, :].bitcast(FP8),
+                                            scalar1=q_scale[:, g, t:t + 1], scalar2=None, op0=ALU.mult)
+                else:
+                    nc.scalar.activation(out=unit_wide[:, t, :], in_=byte_rows[(pos, g)][:, t, :].bitcast(FP8),
+                                         func=ACT.Copy, scale=q_scale[:, g, t:t + 1])
             bf16_rows[(pos, g)] = unit_wide
 
-        def interleave(pos, g):
-            if g < VECTOR_UNITS[pos]:
+        def interleave(pos, g, early=False):
+            if (pos, g) in grouped:
+                return
+            if early:
+                unit_grouped = side_by_side.tile([P, NCH, PACK], BF16, tag="by_scalar", align_bytes=64)
+                copy = nc.vector.tensor_copy
+            elif g < VECTOR_UNITS[pos]:
                 unit_grouped = side_by_side.tile([P, NCH, PACK], BF16, tag="by_vector", align_bytes=64, bufs=VECTOR_BUFS)
                 copy = nc.vector.tensor_copy
             else:
@@ -186,23 +196,29 @@ def tile_multiscaleretention_pa_kernel(tc, x, w_q_bytes, w_q_scale, w_k, out_0, 
                 if m != LATE_TILE or pos == CHUNKS - 1:
                     add_and_store(pos, m)
 
-        def vector_prepares(pos):
+        def vector_prepares(pos, adds_of=None):
             first = VECTOR_UNITS[pos]
             waiting = list(range(first + TENSOR_UNITS[pos], PASSES)) + list(range(first, first + TENSOR_UNITS[pos]))
             for g in range(VECTOR_UNITS[pos]):
                 interleave(pos, g)
+                if g == 0 and adds_of is not None:
+                    vector_adds(adds_of)
+                    adds_of = None
                 if waiting:
                     quantize(pos, waiting.pop(0))
                 waiting.append(g)
+            if adds_of is not None:
+                quantize(pos, waiting.pop(0))
+                vector_adds(adds_of)
             return waiting
 
-        def prepare(pos):
+        def prepare(pos, adds_of=None):
             if pos + 2 < CHUNKS:
                 load(pos + 2, 0)
                 load(pos + 2, 1)
             if 1 <= pos < CHUNKS - 1:
                 scalar_prepares(pos + 1)
-            waiting = vector_prepares(pos)
+            waiting = vector_prepares(pos, adds_of)
             if pos + 2 < CHUNKS:
                 load(pos + 2, 2)
                 load(pos + 2, 3)
@@ -248,18 +264,25 @@ def tile_multiscaleretention_pa_kernel(tc, x, w_q_bytes, w_q_scale, w_k, out_0, 
             nc.scalar.activation(out=ln_d[:], in_=ln_d[:], func=ACT.Ln, scale=2.0 / (1.4 * C), bias=0.4 * C / (1.4 * C))
 
             freq = const.tile([P, PAIRS], F32, name="freq")
-            nc.vector.memset(freq[:, 0:1], 1.0)
+            fine = head.tile([P, 32], F32, name="fine", bufs=1)
+            coarse = head.tile([P, 32], F32, name="coarse", bufs=1)
+            nc.vector.memset(fine[:, 0:1], 1.0)
+            nc.vector.memset(coarse[:, 0:1], 1.0)
             token_turns = const.tile([P, TILES], F32, name="token_turns")
             token_512th = const.tile([P, TILES], F32, name="token_512th")
             token_minus = const.tile([P, TILES], F32, name="token_minus")
-            per_token = {4: (token_512th, 1.0 / 512.0), 5: (token_turns, 1.0 / (2.0 * math.pi)), 6: (token_minus, -1.0)}
-            for level in range(10):
+            for level in range(5):
                 w = 1 << level
-                nc.vector.tensor_scalar(out=freq[:, w:2 * w], in0=freq[:, 0:w],
+                nc.vector.tensor_scalar(out=fine[:, w:2 * w], in0=fine[:, 0:w],
                                         scalar1=pow(10000.0, -w / float(PAIRS)), scalar2=None, op0=ALU.mult)
-                if level in per_token:
-                    nc.vector.tensor_scalar(out=per_token[level][0][:], in0=token[:], scalar1=per_token[level][1],
-                                            scalar2=None, op0=ALU.mult)
+                nc.vector.tensor_scalar(out=coarse[:, w:2 * w], in0=coarse[:, 0:w],
+                                        scalar1=pow(10000.0, -32 * w / float(PAIRS)), scalar2=None, op0=ALU.mult)
+            nc.vector.tensor_scalar(out=token_512th[:], in0=token[:], scalar1=1.0 / 512.0, scalar2=None, op0=ALU.mult)
+            nc.vector.tensor_tensor(out=freq[:].rearrange("p (a b) -> p a b", b=32),
+                                    in0=coarse[:].unsqueeze(2).to_broadcast([P, 32, 32]),
+                                    in1=fine[:].unsqueeze(1).to_broadcast([P, 32, 32]), op=ALU.mult)
+            nc.vector.tensor_scalar(out=token_turns[:], in0=token[:], scalar1=1.0 / (2.0 * math.pi), scalar2=None, op0=ALU.mult)
+            nc.vector.tensor_scalar(out=token_minus[:], in0=token[:], scalar1=-1.0, scalar2=None, op0=ALU.mult)
 
             cos_table = []
             sin_table = []
@@ -276,15 +299,13 @@ def tile_multiscaleretention_pa_kernel(tc, x, w_q_bytes, w_q_scale, w_k, out_0, 
             reduced = max(small)
             wholes = []
             parts = []
-            for step in range(TILES + 1):
-                if step < TILES:
-                    m = step
+            for first in (0, 2):
+                for m in (first, first + 1):
                     whole = head.tile([P, reduced], I32, tag="whole")
                     nc.vector.tensor_scalar(out=whole[:, 0:small[m]], in0=freq[:, 0:small[m]],
                                             scalar1=token_turns[:, m:m + 1], scalar2=None, op0=ALU.mult)
                     wholes.append(whole)
-                if step >= 1:
-                    m = step - 1
+                for m in (first, first + 1):
                     part = head.tile([P, reduced], F32, name="part%d" % m, bufs=1)
                     nc.vector.scalar_tensor_tensor(out=part[:, 0:small[m]], in0=freq[:, 0:small[m]],
                                                    scalar=token_turns[:, m:m + 1], in1=wholes[m][:, 0:small[m]],
@@ -321,12 +342,14 @@ def tile_multiscaleretention_pa_kernel(tc, x, w_q_bytes, w_q_scale, w_k, out_0, 
                 nc.scalar.activation(out=cos_a[:, 0:s], in_=size[:, 0:s], func=ACT.Sin, scale=-2.0 * math.pi,
                                      bias=0.5 * math.pi)
 
-            def finish_tables(m):
-                table_c, table_s = cos_table[m], sin_table[m]
-                nc.vector.tensor_tensor(out=table_s[:, 1, :], in0=table_s[:, 1, :], in1=table_c[:], op=ALU.mult)
-                nc.vector.tensor_tensor(out=table_c[:], in0=table_s[:, 0, :], in1=table_c[:], op=ALU.mult)
-                nc.vector.tensor_scalar(out=table_s[:, 0, :], in0=table_s[:, 1, :], scalar1=-1.0, scalar2=None,
-                                        op0=ALU.mult)
+            def finish_tables(tiles):
+                for m in tiles:
+                    nc.vector.tensor_tensor(out=sin_table[m][:, 1, :], in0=sin_table[m][:, 1, :], in1=cos_table[m][:], op=ALU.mult)
+                for m in tiles:
+                    nc.vector.tensor_tensor(out=cos_table[m][:], in0=sin_table[m][:, 0, :], in1=cos_table[m][:], op=ALU.mult)
+                for m in tiles:
+                    nc.vector.tensor_scalar(out=sin_table[m][:, 0, :], in0=sin_table[m][:, 1, :], scalar1=-1.0, scalar2=None,
+                                            op0=ALU.mult)
 
             for m in range(TILES):
                 sines(m)
@@ -342,21 +365,19 @@ def tile_multiscaleretention_pa_kernel(tc, x, w_q_bytes, w_q_scale, w_k, out_0, 
                 x_scales.append(tile_scales)
             for g in waiting:
                 quantize(0, g)
-            finish_tables(0)
-            finish_tables(1)
+            interleave(2, 0, early=True)
+            finish_tables((0, 1))
             scalar_prepares(1)
             for m in range(TILES):
                 multiply(0, m)
-            finish_tables(2)
-            finish_tables(3)
+            finish_tables((2, 3))
             for g in prepare(1):
                 quantize(1, g)
 
         xpos_tiles.append(ctx.enter_context(tc.tile_pool(name="xpos_tiles", bufs=XPOS_BUFS)))
         rotate(0, True)
         for pos in range(2, CHUNKS - 1):
-            vector_adds(pos - 2)
-            for g in prepare(pos):
+            for g in prepare(pos, pos - 2):
                 quantize(pos, g)
             rotate(pos - 1, True)
         last = CHUNKS - 1

@@ -28,7 +28,7 @@ CHUNKS = 2 * C // NCH
 PAIRS = C // 2
 JCH = NCH // 2
 
-VECTOR_UNITS = (4, 4, 1, 1, 1, 1, 1, 0)
+VECTOR_UNITS = (4, 4, 2, 1, 1, 1, 1, 0)
 
 TENSOR_UNITS = (0, 0, 2, 2, 1, 2, 1, 2)
 
@@ -75,6 +75,8 @@ def tile_multiscaleretention_pa_kernel(tc, x, w_q_bytes, w_q_scale, w_k, out_0, 
             return slice((pos // 2) * NCH, (pos // 2 + 1) * NCH)
 
         def load(pos, g):
+            if (pos, g) in bf16_rows:
+                return
             k_rows = slice(g * K_PASS, (g + 1) * K_PASS)
             if is_q(pos):
                 unit_bytes = rows_q.tile([P, PACK, NCH], U8, tag="unit_bytes")
@@ -248,14 +250,15 @@ def tile_multiscaleretention_pa_kernel(tc, x, w_q_bytes, w_q_scale, w_k, out_0, 
                     nc.sync.dma_start(out=x_rows[m][:], in_=x[0, m * P:(m + 1) * P, :])
             q_scale = const.tile([P, PASSES, PACK], F32, name="q_scale")
             nc.sync.dma_start(out=q_scale[:], in_=w_q_scale.rearrange("(g p t) o -> p g (t o)", p=P, t=PACK))
+            load(2, 0)
             for g in range(PASSES):
                 load(1, g)
 
-            ln_d = head.tile([P, PAIRS], F32, name="ln_d", bufs=1)
-            nc.gpsimd.iota(ln_d[:], pattern=[[1, PAIRS]], base=0, channel_multiplier=0,
-                           allow_small_or_imprecise_dtypes=True)
             token = const.tile([P, TILES], F32, name="token")
             nc.gpsimd.iota(token[:], pattern=[[P, TILES]], base=0, channel_multiplier=1,
+                           allow_small_or_imprecise_dtypes=True)
+            ln_d = head.tile([P, PAIRS], F32, name="ln_d", bufs=1)
+            nc.gpsimd.iota(ln_d[:], pattern=[[1, PAIRS]], base=0, channel_multiplier=0,
                            allow_small_or_imprecise_dtypes=True)
             identity = const.tile([P, P], F32, name="identity")
             make_identity(nc, identity[:])
@@ -313,7 +316,8 @@ def tile_multiscaleretention_pa_kernel(tc, x, w_q_bytes, w_q_scale, w_k, out_0, 
                     parts.append(part)
 
             x_grouped = []
-            for m in range(TILES):
+
+            def turn_tokens(m):
                 words = x_rows[m][:].bitcast(F32)
                 tile_grouped = head.tile([P, PASSES * P * PACK], BF16, name="x_grouped%d" % m, bufs=1, align_bytes=64)
                 as_words = tile_grouped[:].bitcast(F32).rearrange("p (g r u) -> p g r u", g=PASSES, r=P, u=2)
@@ -351,22 +355,31 @@ def tile_multiscaleretention_pa_kernel(tc, x, w_q_bytes, w_q_scale, w_k, out_0, 
                     nc.vector.tensor_scalar(out=sin_table[m][:, 0, :], in0=sin_table[m][:, 1, :], scalar1=-1.0, scalar2=None,
                                             op0=ALU.mult)
 
-            for m in range(TILES):
-                sines(m)
+            for first in (0, 2):
+                for m in (first, first + 1):
+                    turn_tokens(m)
+                for m in (first, first + 1):
+                    sines(m)
 
             waiting = prepare(0)
             x_codes = []
             x_scales = []
-            for m in range(TILES):
+
+            def quantize_tokens(m):
                 tile_codes = const.tile([P, PASSES * P], U32, name="x_codes%d" % m, align_bytes=64)
                 tile_scales = const.tile([P, PASSES * P], U8, name="x_scales%d" % m, align_bytes=64)
                 nc.vector.quantize_mx(out=tile_codes[:].bitcast(FP8X4), scales=tile_scales[:], in_=x_grouped[m][:])
                 x_codes.append(tile_codes)
                 x_scales.append(tile_scales)
+
+            quantize_tokens(0)
+            quantize_tokens(1)
             for g in waiting:
                 quantize(0, g)
             interleave(2, 0, early=True)
             finish_tables((0, 1))
+            quantize_tokens(2)
+            quantize_tokens(3)
             scalar_prepares(1)
             for m in range(TILES):
                 multiply(0, m)

@@ -33,6 +33,7 @@ VECTOR_UNITS = (4, 4, 2, 1, 1, 1, 1, 0)
 TENSOR_UNITS = (0, 0, 2, 2, 1, 2, 1, 2)
 
 GPSIMD_TILES = 2
+WARM_UP = 8
 WIDENED_BY_VECTOR = 0
 LATE_TILE = 2
 
@@ -142,8 +143,13 @@ def tile_multiscaleretention_pa_kernel(tc, x, w_q_bytes, w_q_scale, w_k, out_0, 
                                   in_=grouped[(pos, g)][:].rearrange("p c t -> p (c t)"))
             w_codes[(pos, g)] = (codes, scales)
 
-        def multiply(pos, m):
+        def multiply(pos, m, warm_up=0):
             bank = psum.tile([P, NCH], F32, tag="bank", bufs=SUM_BANKS)
+            for n in range(warm_up):
+                codes, scales = w_codes[(pos - 1, n % PASSES)]
+                nc.tensor.matmul_mx(out=bank[:],
+                                    lhsT=x_codes[m][:, 0:P].bitcast(FP8X4), lhsT_scale=x_scales[m][:, 0:P],
+                                    rhs=codes[:].bitcast(FP8X4), rhs_scale=scales[:], start=True, stop=True)
             for g in range(PASSES):
                 codes, scales = w_codes[(pos, g)]
                 nc.tensor.matmul_mx(out=bank[:],
@@ -399,7 +405,7 @@ def tile_multiscaleretention_pa_kernel(tc, x, w_q_bytes, w_q_scale, w_k, out_0, 
         for g in prepare(last):
             quantize(last, g)
         for m in range(TILES):
-            multiply(last, m)
+            multiply(last, m, WARM_UP if m == 0 else 0)
         vector_adds(last - 1)
         rotate(last, False)
         vector_adds(last)

@@ -24,13 +24,14 @@ K_PASS = P * PACK
 PASSES = E // K_PASS
 TILES = T // P
 NCH = 512
-CHUNKS = 2 * C // NCH
+CHUNK = ((False, 0, 512), (True, 0, 512), (False, 512, 512), (True, 512, 512), (False, 1024, 512), (True, 1024, 512), (False, 1536, 512), (True, 1536, 256), (True, 1792, 256))
+CHUNKS = len(CHUNK)
 PAIRS = C // 2
 JCH = NCH // 2
 
-VECTOR_UNITS = (4, 4, 2, 1, 1, 1, 1, 0)
+VECTOR_UNITS = (4, 4, 2, 1, 1, 1, 0, 0, 0)
 
-TENSOR_UNITS = (0, 0, 2, 2, 1, 2, 1, 2)
+TENSOR_UNITS = (0, 0, 2, 2, 1, 2, 1, 2, 2)
 
 GPSIMD_TILES = 2
 WARM_UP = 8
@@ -70,28 +71,35 @@ def tile_multiscaleretention_pa_kernel(tc, x, w_q_bytes, w_q_scale, w_k, out_0, 
         xpos_tiles = []
 
         def is_q(pos):
-            return pos % 2 == 1
+            return CHUNK[pos][0]
+
+        def width(pos):
+            return CHUNK[pos][2]
 
         def channels(pos):
-            return slice((pos // 2) * NCH, (pos // 2 + 1) * NCH)
+            return slice(CHUNK[pos][1], CHUNK[pos][1] + CHUNK[pos][2])
 
         def load(pos, g):
-            if (pos, g) in bf16_rows:
+            from_q, first, columns = CHUNK[pos]
+            if first % NCH != 0 or (pos, g) in bf16_rows or (pos, g) in byte_rows:
                 return
             k_rows = slice(g * K_PASS, (g + 1) * K_PASS)
-            if is_q(pos):
-                unit_bytes = rows_q.tile([P, PACK, NCH], U8, tag="unit_bytes")
-                nc.sync.dma_start(out=unit_bytes[:],
-                                  in_=w_q_bytes[k_rows, channels(pos)].rearrange("(p t) n -> p t n", t=PACK))
-                byte_rows[(pos, g)] = unit_bytes
+            if from_q:
+                unit = rows_q.tile([P, PACK, NCH], U8, tag="unit_bytes")
+                nc.sync.dma_start(out=unit[:], in_=w_q_bytes[k_rows, first:first + NCH].rearrange("(p t) n -> p t n", t=PACK))
             else:
-                unit_rows = rows_k.tile([P, PACK, NCH], BF16, tag="unit_rows")
-                nc.sync.dma_start(out=unit_rows[:],
-                                  in_=w_k[k_rows, channels(pos)].rearrange("(p t) n -> p t n", t=PACK))
-                bf16_rows[(pos, g)] = unit_rows
+                unit = rows_k.tile([P, PACK, NCH], BF16, tag="unit_rows")
+                nc.sync.dma_start(out=unit[:], in_=w_k[k_rows, first:first + NCH].rearrange("(p t) n -> p t n", t=PACK))
+            for other in range(CHUNKS):
+                if CHUNK[other][0] == from_q and first <= CHUNK[other][1] < first + NCH:
+                    view = unit[:, :, CHUNK[other][1] - first:CHUNK[other][1] - first + CHUNK[other][2]]
+                    if from_q:
+                        byte_rows[(other, g)] = view
+                    else:
+                        bf16_rows[(other, g)] = view
 
         def widen(pos, g):
-            unit_wide = widened.tile([P, PACK, NCH], BF16, tag="unit_wide")
+            unit_wide = widened.tile([P, PACK, width(pos)], BF16, tag="unit_wide")
             for t in range(PACK):
                 if pos == 1 and g >= PASSES - WIDENED_BY_VECTOR:
                     nc.vector.tensor_scalar(out=unit_wide[:, t, :], in0=byte_rows[(pos, g)][:, t, :].bitcast(FP8),
@@ -105,13 +113,13 @@ def tile_multiscaleretention_pa_kernel(tc, x, w_q_bytes, w_q_scale, w_k, out_0, 
             if (pos, g) in grouped:
                 return
             if early:
-                unit_grouped = side_by_side.tile([P, NCH, PACK], BF16, tag="by_scalar", align_bytes=64)
+                unit_grouped = side_by_side.tile([P, width(pos), PACK], BF16, tag="by_scalar", align_bytes=64)
                 copy = nc.vector.tensor_copy
             elif g < VECTOR_UNITS[pos]:
-                unit_grouped = side_by_side.tile([P, NCH, PACK], BF16, tag="by_vector", align_bytes=64, bufs=VECTOR_BUFS)
+                unit_grouped = side_by_side.tile([P, width(pos), PACK], BF16, tag="by_vector", align_bytes=64, bufs=VECTOR_BUFS)
                 copy = nc.vector.tensor_copy
             else:
-                unit_grouped = side_by_side.tile([P, NCH, PACK], BF16, tag="by_scalar", align_bytes=64)
+                unit_grouped = side_by_side.tile([P, width(pos), PACK], BF16, tag="by_scalar", align_bytes=64)
                 copy = nc.scalar.copy
             copy(out=unit_grouped[:].rearrange("p (c i) t -> p c t i", i=4),
                  in_=bf16_rows[(pos, g)][:].rearrange("p t (c i) -> p c t i", i=4))
@@ -119,32 +127,34 @@ def tile_multiscaleretention_pa_kernel(tc, x, w_q_bytes, w_q_scale, w_k, out_0, 
 
         def pass_through(pos, g):
             banks = []
-            for half in range(2):
-                bank = psum.tile([P, 2 * NCH], BF16, tag="through", bufs=THROUGH_BANKS)
-                for quarter in range(2):
-                    c0 = (2 * half + quarter) * P
-                    nc.tensor.matmul(out=bank[:, quarter * NCH:(quarter + 1) * NCH].rearrange("p (c t) -> p t c", t=PACK),
-                                     lhsT=identity_bf16[:], rhs=bf16_rows[(pos, g)][:, :, c0:c0 + P],
-                                     start=True, stop=True)
-                banks.append(bank)
+            for c0 in range(0, width(pos), P):
+                if c0 % (2 * P) == 0:
+                    bank = psum.tile([P, 2 * NCH], BF16, tag="through", bufs=THROUGH_BANKS)
+                    banks.append(bank)
+                quarter = (c0 // P) % 2
+                nc.tensor.matmul(out=bank[:, quarter * NCH:(quarter + 1) * NCH].rearrange("p (c t) -> p t c", t=PACK),
+                                 lhsT=identity_bf16[:], rhs=bf16_rows[(pos, g)][:, :, c0:c0 + P],
+                                 start=True, stop=True)
             passed[(pos, g)] = banks
 
         def empty_through(pos, g):
-            unit_grouped = side_by_side.tile([P, NCH, PACK], BF16, tag="by_scalar", align_bytes=64)
+            unit_grouped = side_by_side.tile([P, width(pos), PACK], BF16, tag="by_scalar", align_bytes=64)
             flat = unit_grouped[:].rearrange("p c t -> p (c t)")
-            for half in range(2):
-                nc.scalar.copy(out=flat[:, half * 2 * NCH:(half + 1) * 2 * NCH], in_=passed[(pos, g)][half][:])
+            for half in range(len(passed[(pos, g)])):
+                count = min(2 * NCH, PACK * width(pos) - half * 2 * NCH)
+                nc.scalar.copy(out=flat[:, half * 2 * NCH:half * 2 * NCH + count].bitcast(F32),
+                               in_=passed[(pos, g)][half][:, 0:count].bitcast(F32))
             grouped[(pos, g)] = unit_grouped
 
         def quantize(pos, g):
-            codes = quantized.tile([P, NCH], U32, tag="codes", align_bytes=64)
-            scales = quantized.tile([P, NCH], U8, tag="scales", align_bytes=64)
+            codes = quantized.tile([P, width(pos)], U32, tag="codes", align_bytes=64)
+            scales = quantized.tile([P, width(pos)], U8, tag="scales", align_bytes=64)
             nc.vector.quantize_mx(out=codes[:].bitcast(FP8X4), scales=scales[:],
                                   in_=grouped[(pos, g)][:].rearrange("p c t -> p (c t)"))
             w_codes[(pos, g)] = (codes, scales)
 
         def multiply(pos, m, warm_up=0):
-            bank = psum.tile([P, NCH], F32, tag="bank", bufs=SUM_BANKS)
+            bank = psum.tile([P, width(pos)], F32, tag="bank", bufs=SUM_BANKS)
             for n in range(warm_up):
                 codes, scales = w_codes[(pos - 1, n % PASSES)]
                 nc.tensor.matmul_mx(out=bank[:],
@@ -160,13 +170,14 @@ def tile_multiscaleretention_pa_kernel(tc, x, w_q_bytes, w_q_scale, w_k, out_0, 
             sums[(pos, m)] = bank
 
         def make_products(pos, m):
-            pairs = slice((pos // 2) * JCH, (pos // 2 + 1) * JCH)
+            pairs = slice(CHUNK[pos][1] // 2, (CHUNK[pos][1] + CHUNK[pos][2]) // 2)
+            count = width(pos) // 2
             z = sums[(pos, m)][:].rearrange("p (j e) -> p j e", e=2)
             pool = xpos_tiles[0]
-            by_cos = pool.tile([P, JCH, 2], F32, tag="by_cos")
+            by_cos = pool.tile([P, count, 2], F32, tag="by_cos")
             nc.vector.tensor_tensor(out=by_cos[:], in0=z,
-                                    in1=cos_table[m][:, pairs].unsqueeze(2).to_broadcast([P, JCH, 2]), op=ALU.mult)
-            by_sin = pool.tile([P, JCH, 2], F32, tag="by_sin")
+                                    in1=cos_table[m][:, pairs].unsqueeze(2).to_broadcast([P, count, 2]), op=ALU.mult)
+            by_sin = pool.tile([P, count, 2], F32, tag="by_sin")
             nc.vector.tensor_tensor(out=by_sin[:], in0=z[:, :, ::-1],
                                     in1=sin_table[m][:, :, pairs].rearrange("p e j -> p j e"), op=ALU.mult)
             products[(pos, m)] = (by_cos, by_sin)
@@ -174,7 +185,7 @@ def tile_multiscaleretention_pa_kernel(tc, x, w_q_bytes, w_q_scale, w_k, out_0, 
         def add_and_store(pos, m):
             by_cos, by_sin = products[(pos, m)]
             pool = xpos_tiles[0]
-            rotated = pool.tile([P, NCH], F32, tag="rotated")
+            rotated = pool.tile([P, width(pos)], F32, tag="rotated")
             engine = nc.gpsimd if m < GPSIMD_TILES or (m == LATE_TILE and pos < CHUNKS - 1) else nc.vector
             engine.tensor_tensor(out=rotated[:], in0=by_cos[:].rearrange("p j e -> p (j e)"),
                                  in1=by_sin[:].rearrange("p j e -> p (j e)"), op=ALU.add)

from contextlib import ExitStack
import math

import concourse.mybir as mybir
from concourse.masks import make_identity

T, E, C = 512, 2048, 2048
FLOPS = 2 * 2 * T * E * C

F32 = mybir.dt.float32
BF16 = mybir.dt.bfloat16
U32 = mybir.dt.uint32
I32 = mybir.dt.int32
U8 = mybir.dt.uint8
FP8 = mybir.dt.float8_e4m3fn
FP8X4 = mybir.dt.float8_e4m3fn_x4
ACT = mybir.ActivationFunctionType
ALU = mybir.AluOpType
ENG = mybir.EngineType

P = 128
PACK = 4
K_PASS = P * PACK
PASSES = E // K_PASS
TILES = T // P
NCH = 512
CHUNK = ((False, 0, 512), (True, 0, 512), (False, 512, 512), (True, 512, 512), (False, 1024, 512), (True, 1024, 512), (False, 1536, 512), (True, 1536, 256), (True, 1792, 256))
CHUNKS = len(CHUNK)
PAIRS = C // 2
JCH = NCH // 2

VECTOR_UNITS = (4, 4, 2, 1, 1, 1, 0, 0, 0)

TENSOR_UNITS = (0, 0, 2, 2, 1, 2, 1, 2, 2)

GPSIMD_TILES = 2
WARM_UP = 8
WIDENED_BY_VECTOR = 0
LATE_TILE = 2

SUM_BANKS = 4
THROUGH_BANKS = 4

RAW_BUFS = 6
WIDE_BUFS = 4
SCALAR_BUFS = 8
VECTOR_BUFS = 3
CODE_BUFS = 8
XPOS_BUFS = 6


def tile_multiscaleretention_pa_kernel(tc, x, w_q_bytes, w_q_scale, w_k, out_0, out_1):
    nc = tc.nc
    with ExitStack() as ctx:
        ctx.enter_context(tc.manual_schedule(engines={ENG.DVE, ENG.Pool, ENG.Activation, ENG.PE}))
        const = ctx.enter_context(tc.tile_pool(name="const", bufs=1))
        rows_k = ctx.enter_context(tc.tile_pool(name="rows_k", bufs=RAW_BUFS))
        rows_q = ctx.enter_context(tc.tile_pool(name="rows_q", bufs=RAW_BUFS))
        widened = ctx.enter_context(tc.tile_pool(name="widened", bufs=WIDE_BUFS))
        side_by_side = ctx.enter_context(tc.tile_pool(name="side_by_side", bufs=SCALAR_BUFS))
        quantized = ctx.enter_context(tc.tile_pool(name="quantized", bufs=CODE_BUFS))
        psum = ctx.enter_context(tc.psum_pool(name="psum", bufs=SUM_BANKS))

        byte_rows = {}
        bf16_rows = {}
        grouped = {}
        passed = {}
        w_codes = {}
        sums = {}
        products = {}
        xpos_tiles = []

        def is_q(pos):
            return CHUNK[pos][0]

        def width(pos):
            return CHUNK[pos][2]

        def channels(pos):
            return slice(CHUNK[pos][1], CHUNK[pos][1] + CHUNK[pos][2])

        def load(pos, g):
            from_q, first, columns = CHUNK[pos]
            if first % NCH != 0 or (pos, g) in bf16_rows or (pos, g) in byte_rows:
                return
            k_rows = slice(g * K_PASS, (g + 1) * K_PASS)
            if from_q:
                unit = rows_q.tile([P, PACK, NCH], U8, tag="unit_bytes")
                nc.sync.dma_start(out=unit[:], in_=w_q_bytes[k_rows, first:first + NCH].rearrange("(p t) n -> p t n", t=PACK))
            else:
                unit = rows_k.tile([P, PACK, NCH], BF16, tag="unit_rows")
                nc.sync.dma_start(out=unit[:], in_=w_k[k_rows, first:first + NCH].rearrange("(p t) n -> p t n", t=PACK))
            for other in range(CHUNKS):
                if CHUNK[other][0] == from_q and first <= CHUNK[other][1] < first + NCH:
                    view = unit[:, :, CHUNK[other][1] - first:CHUNK[other][1] - first + CHUNK[other][2]]
                    if from_q:
                        byte_rows[(other, g)] = view
                    else:
                        bf16_rows[(other, g)] = view

        def widen(pos, g):
            unit_wide = widened.tile([P, PACK, width(pos)], BF16, tag="unit_wide")
            for t in range(PACK):
                if pos == 1 and g >= PASSES - WIDENED_BY_VECTOR:
                    nc.vector.tensor_scalar(out=unit_wide[:, t, :], in0=byte_rows[(pos, g)][:, t, :].bitcast(FP8),
                                            scalar1=q_scale[:, g, t:t + 1], scalar2=None, op0=ALU.mult)
                else:
                    nc.scalar.activation(out=unit_wide[:, t, :], in_=byte_rows[(pos, g)][:, t, :].bitcast(FP8),
                                         func=ACT.Copy, scale=q_scale[:, g, t:t + 1])
            bf16_rows[(pos, g)] = unit_wide

        def interleave(pos, g, early=False):
            if (pos, g) in grouped:
                return
            if early:
                unit_grouped = side_by_side.tile([P, width(pos), PACK], BF16, tag="by_scalar", align_bytes=64)
                copy = nc.vector.tensor_copy
            elif g < VECTOR_UNITS[pos]:
                unit_grouped = side_by_side.tile([P, width(pos), PACK], BF16, tag="by_vector", align_bytes=64, bufs=VECTOR_BUFS)
                copy = nc.vector.tensor_copy
            else:
                unit_grouped = side_by_side.tile([P, width(pos), PACK], BF16, tag="by_scalar", align_bytes=64)
                copy = nc.scalar.copy
            copy(out=unit_grouped[:].rearrange("p (c i) t -> p c t i", i=4),
                 in_=bf16_rows[(pos, g)][:].rearrange("p t (c i) -> p c t i", i=4))
            grouped[(pos, g)] = unit_grouped

        def pass_through(pos, g):
            banks = []
            for c0 in range(0, width(pos), P):
                if c0 % (2 * P) == 0:
                    bank = psum.tile([P, 2 * NCH], BF16, tag="through", bufs=THROUGH_BANKS)
                    banks.append(bank)
                quarter = (c0 // P) % 2
                nc.tensor.matmul(out=bank[:, quarter * NCH:(quarter + 1) * NCH].rearrange("p (c t) -> p t c", t=PACK),
                                 lhsT=identity_bf16[:], rhs=bf16_rows[(pos, g)][:, :, c0:c0 + P],
                                 start=True, stop=True)
            passed[(pos, g)] = banks

        def empty_through(pos, g):
            unit_grouped = side_by_side.tile([P, width(pos), PACK], BF16, tag="by_scalar", align_bytes=64)
            flat = unit_grouped[:].rearrange("p c t -> p (c t)")
            for half in range(len(passed[(pos, g)])):
                count = min(2 * NCH, PACK * width(pos) - half * 2 * NCH)
                nc.scalar.copy(out=flat[:, half * 2 * NCH:half * 2 * NCH + count].bitcast(F32),
                               in_=passed[(pos, g)][half][:, 0:count].bitcast(F32))
            grouped[(pos, g)] = unit_grouped

        def quantize(pos, g):
            codes = quantized.tile([P, width(pos)], U32, tag="codes", align_bytes=64)
            scales = quantized.tile([P, width(pos)], U8, tag="scales", align_bytes=64)
            nc.vector.quantize_mx(out=codes[:].bitcast(FP8X4), scales=scales[:],
                                  in_=grouped[(pos, g)][:].rearrange("p c t -> p (c t)"))
            w_codes[(pos, g)] = (codes, scales)

        def multiply(pos, m, warm_up=0):
            bank = psum.tile([P, width(pos)], F32, tag="bank", bufs=SUM_BANKS)
            for n in range(warm_up):
                codes, scales = w_codes[(pos - 1, n % PASSES)]
                nc.tensor.matmul_mx(out=bank[:],
                                    lhsT=x_codes[m][:, 0:P].bitcast(FP8X4), lhsT_scale=x_scales[m][:, 0:P],
                                    rhs=codes[:].bitcast(FP8X4), rhs_scale=scales[:], start=True, stop=True)
            for g in range(PASSES):
                codes, scales = w_codes[(pos, g)]
                nc.tensor.matmul_mx(out=bank[:],
                                    lhsT=x_codes[m][:, g * P:(g + 1) * P].bitcast(FP8X4),
                                    lhsT_scale=x_scales[m][:, g * P:(g + 1) * P],
                                    rhs=codes[:].bitcast(FP8X4), rhs_scale=scales[:],
                                    start=(g == 0), stop=(g == PASSES - 1))
            sums[(pos, m)] = bank

        def make_products(pos, m):
            pairs = slice(CHUNK[pos][1] // 2, (CHUNK[pos][1] + CHUNK[pos][2]) // 2)
            count = width(pos) // 2
            z = sums[(pos, m)][:].rearrange("p (j e) -> p j e", e=2)
            pool = xpos_tiles[0]
            by_cos = pool.tile([P, count, 2], F32, tag="by_cos")
            nc.vector.tensor_tensor(out=by_cos[:], in0=z,
                                    in1=cos_table[m][:, pairs].unsqueeze(2).to_broadcast([P, count, 2]), op=ALU.mult)
            by_sin = pool.tile([P, count, 2], F32, tag="by_sin")
            nc.vector.tensor_tensor(out=by_sin[:], in0=z[:, :, ::-1],
                                    in1=sin_table[m][:, :, pairs].rearrange("p e j -> p j e"), op=ALU.mult)
            products[(pos, m)] = (by_cos, by_sin)

        def add_and_store(pos, m):
            by_cos, by_sin = products[(pos, m)]
            pool = xpos_tiles[0]
            rotated = pool.tile([P, width(pos)], F32, tag="rotated")
            engine = nc.gpsimd if m < GPSIMD_TILES or (m == LATE_TILE and pos < CHUNKS - 1) else nc.vector
            engine.tensor_tensor(out=rotated[:], in0=by_cos[:].rearrange("p j e -> p (j e)"),
                                 in1=by_sin[:].rearrange("p j e -> p (j e)"), op=ALU.add)
            out = out_0 if is_q(pos) else out_1
            nc.sync.dma_start(out=out[0, m * P:(m + 1) * P, channels(pos)], in_=rotated[:])

        def scalar_prepares(pos):
            first = VECTOR_UNITS[pos]
            by_tensor = list(range(first, first + TENSOR_UNITS[pos]))
            by_scalar = list(range(first + TENSOR_UNITS[pos], PASSES))
            if is_q(pos):
                for g in by_tensor:
                    widen(pos, g)
                    pass_through(pos, g)
                for g in by_scalar + list(range(first)):
                    widen(pos, g)
            else:
                for g in by_tensor:
                    pass_through(pos, g)
            for g in by_scalar:
                interleave(pos, g)
            for g in by_tensor:
                empty_through(pos, g)

        def vector_adds(pos):
            for m in range(GPSIMD_TILES, TILES):
                if m != LATE_TILE or pos == CHUNKS - 1:
                    add_and_store(pos, m)

        def vector_prepares(pos, adds_of=None):
            first = VECTOR_UNITS[pos]
            waiting = list(range(first + TENSOR_UNITS[pos], PASSES)) + list(range(first, first + TENSOR_UNITS[pos]))
            for g in range(VECTOR_UNITS[pos]):
                interleave(pos, g)
                if g == 0 and adds_of is not None:
                    vector_adds(adds_of)
                    adds_of = None
                if waiting:
                    quantize(pos, waiting.pop(0))
                waiting.append(g)
            if adds_of is not None:
                quantize(pos, waiting.pop(0))
                vector_adds(adds_of)
            return waiting

        def prepare(pos, adds_of=None):
            if pos + 2 < CHUNKS:
                load(pos + 2, 0)
                load(pos + 2, 1)
            if 1 <= pos < CHUNKS - 1:
                scalar_prepares(pos + 1)
            waiting = vector_prepares(pos, adds_of)
            if pos + 2 < CHUNKS:
                load(pos + 2, 2)
                load(pos + 2, 3)
            return waiting

        def rotate(pos, then_multiply):
            if pos >= 1:
                late = products[(pos - 1, LATE_TILE)][1]
                nc.vector.tensor_copy(out=late[:, 0:1, :], in_=late[:, 0:1, :])
                add_and_store(pos - 1, LATE_TILE)
            for m in range(TILES):
                make_products(pos, m)
                if 1 <= m <= GPSIMD_TILES:
                    add_and_store(pos, m - 1)
                if then_multiply:
                    multiply(pos + 1, m)

        with tc.tile_pool(name="head", bufs=2) as head:
            x_rows = []
            for m in range(TILES):
                token_rows = head.tile([P, E], BF16, name="token_rows%d" % m, bufs=1)
                x_rows.append(token_rows)
            for half in range(2):
                load(0, 2 * half)
                load(0, 2 * half + 1)
                for m in (2 * half, 2 * half + 1):
                    nc.sync.dma_start(out=x_rows[m][:], in_=x[0, m * P:(m + 1) * P, :])
            q_scale = const.tile([P, PASSES, PACK], F32, name="q_scale")
            nc.sync.dma_start(out=q_scale[:], in_=w_q_scale.rearrange("(g p t) o -> p g (t o)", p=P, t=PACK))
            load(2, 0)
            for g in range(PASSES):
                load(1, g)

            token = const.tile([P, TILES], F32, name="token")
            nc.gpsimd.iota(token[:], pattern=[[P, TILES]], base=0, channel_multiplier=1,
                           allow_small_or_imprecise_dtypes=True)
            ln_d = head.tile([P, PAIRS], F32, name="ln_d", bufs=1)
            nc.gpsimd.iota(ln_d[:], pattern=[[1, PAIRS]], base=0, channel_multiplier=0,
                           allow_small_or_imprecise_dtypes=True)
            identity = const.tile([P, P], F32, name="identity")
            make_identity(nc, identity[:])
            identity_bf16 = const.tile([P, P], BF16, name="identity_bf16")
            make_identity(nc, identity_bf16[:])
            nc.scalar.activation(out=ln_d[:], in_=ln_d[:], func=ACT.Ln, scale=2.0 / (1.4 * C), bias=0.4 * C / (1.4 * C))

            freq = const.tile([P, PAIRS], F32, name="freq")
            fine = head.tile([P, 32], F32, name="fine", bufs=1)
            coarse = head.tile([P, 32], F32, name="coarse", bufs=1)
            nc.vector.memset(fine[:, 0:1], 1.0)
            nc.vector.memset(coarse[:, 0:1], 1.0)
            token_turns = const.tile([P, TILES], F32, name="token_turns")
            token_512th = const.tile([P, TILES], F32, name="token_512th")
            token_minus = const.tile([P, TILES], F32, name="token_minus")
            for level in range(5):
                w = 1 << level
                nc.vector.tensor_scalar(out=fine[:, w:2 * w], in0=fine[:, 0:w],
                                        scalar1=pow(10000.0, -w / float(PAIRS)), scalar2=None, op0=ALU.mult)
                nc.vector.tensor_scalar(out=coarse[:, w:2 * w], in0=coarse[:, 0:w],
                                        scalar1=pow(10000.0, -32 * w / float(PAIRS)), scalar2=None, op0=ALU.mult)
            nc.vector.tensor_scalar(out=token_512th[:], in0=token[:], scalar1=1.0 / 512.0, scalar2=None, op0=ALU.mult)
            nc.vector.tensor_tensor(out=freq[:].rearrange("p (a b) -> p a b", b=32),
                                    in0=coarse[:].unsqueeze(2).to_broadcast([P, 32, 32]),
                                    in1=fine[:].unsqueeze(1).to_broadcast([P, 32, 32]), op=ALU.mult)
            nc.vector.tensor_scalar(out=token_turns[:], in0=token[:], scalar1=1.0 / (2.0 * math.pi), scalar2=None, op0=ALU.mult)
            nc.vector.tensor_scalar(out=token_minus[:], in0=token[:], scalar1=-1.0, scalar2=None, op0=ALU.mult)

            cos_table = []
            sin_table = []
            for m in range(TILES):
                table_c = const.tile([P, PAIRS], F32, name="cos_table%d" % m)
                table_s = const.tile([P, 2, PAIRS], F32, name="sin_table%d" % m)
                cos_table.append(table_c)
                sin_table.append(table_s)
                nc.scalar.activation(out=table_c[:], in_=ln_d[:], func=ACT.Exp, scale=token_512th[:, m:m + 1])

            small = []
            for m in range(TILES):
                small.append(32 * int(math.ceil(PAIRS * math.log((m * P + P - 1) / 3.14) / math.log(10000.0) / 32.0)))
            reduced = max(small)
            wholes = []
            parts = []
            for first in (0, 2):
                for m in (first, first + 1):
                    whole = head.tile([P, reduced], I32, tag="whole")
                    nc.vector.tensor_scalar(out=whole[:, 0:small[m]], in0=freq[:, 0:small[m]],
                                            scalar1=token_turns[:, m:m + 1], scalar2=None, op0=ALU.mult)
                    wholes.append(whole)
                for m in (first, first + 1):
                    part = head.tile([P, reduced], F32, name="part%d" % m, bufs=1)
                    nc.vector.scalar_tensor_tensor(out=part[:, 0:small[m]], in0=freq[:, 0:small[m]],
                                                   scalar=token_turns[:, m:m + 1], in1=wholes[m][:, 0:small[m]],
                                                   op0=ALU.mult, op1=ALU.subtract)
                    parts.append(part)

            x_grouped = []

            def turn_tokens(m):
                words = x_rows[m][:].bitcast(F32)
                tile_grouped = head.tile([P, PASSES * P * PACK], BF16, name="x_grouped%d" % m, bufs=1, align_bytes=64)
                as_words = tile_grouped[:].bitcast(F32).rearrange("p (g r u) -> p g r u", g=PASSES, r=P, u=2)
                for half in range(2):
                    if half == 0:
                        turned = psum.tile([P, 2, 2, P], F32, tag="bank", bufs=SUM_BANKS)
                    else:
                        turned = psum.tile([P, 2, 2, P], F32, tag="through", bufs=THROUGH_BANKS)
                    for gg in range(2):
                        g = 2 * half + gg
                        for u in range(2):
                            nc.tensor.transpose(turned[:, gg, u, :], words[:, 256 * g + u:256 * (g + 1):2], identity[:])
                    nc.scalar.copy(out=as_words[:, 2 * half:2 * half + 2], in_=turned[:].rearrange("p g u r -> p g r u"))
                x_grouped.append(tile_grouped)

            def sines(m):
                s = small[m]
                sin_a = sin_table[m][:, 1, :]
                cos_a = sin_table[m][:, 0, :]
                nc.scalar.activation(out=sin_a[:, s:], in_=freq[:, s:], func=ACT.Sin, scale=token[:, m:m + 1])
                nc.scalar.activation(out=cos_a[:, s:], in_=freq[:, s:], func=ACT.Sin, scale=token_minus[:, m:m + 1],
                                     bias=0.5 * math.pi)
                nc.scalar.activation(out=sin_a[:, 0:s], in_=parts[m][:, 0:s], func=ACT.Sin, scale=2.0 * math.pi)
                size = head.tile([P, reduced], F32, tag="size")
                nc.scalar.activation(out=size[:, 0:s], in_=parts[m][:, 0:s], func=ACT.Abs)
                nc.scalar.activation(out=cos_a[:, 0:s], in_=size[:, 0:s], func=ACT.Sin, scale=-2.0 * math.pi,
                                     bias=0.5 * math.pi)

            def finish_tables(tiles):
                for m in tiles:
                    nc.vector.tensor_tensor(out=sin_table[m][:, 1, :], in0=sin_table[m][:, 1, :], in1=cos_table[m][:], op=ALU.mult)
                for m in tiles:
                    nc.vector.tensor_tensor(out=cos_table[m][:], in0=sin_table[m][:, 0, :], in1=cos_table[m][:], op=ALU.mult)
                for m in tiles:
                    nc.vector.tensor_scalar(out=sin_table[m][:, 0, :], in0=sin_table[m][:, 1, :], scalar1=-1.0, scalar2=None,
                                            op0=ALU.mult)

            for first in (0, 2):
                for m in (first, first + 1):
                    turn_tokens(m)
                for m in (first, first + 1):
                    sines(m)

            waiting = prepare(0)
            x_codes = []
            x_scales = []

            def quantize_tokens(m):
                tile_codes = const.tile([P, PASSES * P], U32, name="x_codes%d" % m, align_bytes=64)
                tile_scales = const.tile([P, PASSES * P], U8, name="x_scales%d" % m, align_bytes=64)
                nc.vector.quantize_mx(out=tile_codes[:].bitcast(FP8X4), scales=tile_scales[:], in_=x_grouped[m][:])
                x_codes.append(tile_codes)
                x_scales.append(tile_scales)

            quantize_tokens(0)
            quantize_tokens(1)
            for g in waiting:
                quantize(0, g)
            interleave(2, 0, early=True)
            finish_tables((0, 1))
            quantize_tokens(2)
            quantize_tokens(3)
            scalar_prepares(1)
            for m in range(TILES):
                multiply(0, m)
            finish_tables((2, 3))
            for g in prepare(1):
                quantize(1, g)

        xpos_tiles.append(ctx.enter_context(tc.tile_pool(name="xpos_tiles", bufs=XPOS_BUFS)))
        rotate(0, True)
        for pos in range(2, CHUNKS - 1):
            for g in prepare(pos, pos - 2):
                quantize(pos, g)
            rotate(pos - 1, True)
        last = CHUNKS - 1
        vector_adds(last - 2)
        rotate(last - 1, False)
        for g in prepare(last):
            quantize(last, g)
        for m in range(TILES):
            multiply(last, m, WARM_UP if m == 0 else 0)
        vector_adds(last - 1)
        rotate(last, False)
        vector_adds(last)
